import numpy as np
import ml_dtypes


def mxq(x, axis, fmt="e4m3"):
    dtype, down = {"e4m3": (ml_dtypes.float8_e4m3fn, 7), "e5m2": (ml_dtypes.float8_e5m2, 14)}[fmt]
    v = np.moveaxis(np.asarray(x, np.float32).astype(ml_dtypes.bfloat16).astype(np.float64), axis, -1)
    blocks = v.reshape(v.shape[:-1] + (-1, 32))
    amax = np.abs(blocks).max(-1, keepdims=True)
    byte = np.maximum(np.where(amax > 0, np.frexp(amax)[1] - 1 + 127, 0) - down, 1)
    scale = np.exp2(byte - 127.0)
    codes = (blocks / scale).astype(np.float32).astype(dtype).astype(np.float64)
    return np.moveaxis((codes * scale).reshape(v.shape), -1, axis)


WIDE = False


def mx_kscale(k):
    if not WIDE:
        return np.ones(k)
    levels = np.array([10, -10, 5, -5, 0])
    a = np.random.permutation(np.resize(levels, k // 512 * 4)).reshape(k // 512, 4)
    idx = np.arange(k)
    return np.exp2(a[idx // 512, idx % 128 // 32])


BF16 = ml_dtypes.bfloat16


def bf(x):
    return np.asarray(x, np.float32).astype(BF16)


def f64(x):
    return np.asarray(x).astype(np.float64)


E2M1 = np.array([0.0, 0.5, 1.0, 1.5, 2.0, 3.0, 4.0, 6.0, -0.0, -0.5, -1.0, -1.5, -2.0, -3.0, -4.0, -6.0])


def pack_weight(w, fmt):
    k, n = w.shape
    w = f64(bf(w)).reshape(k // 32, 32, n)
    amax = np.abs(w).max(1)
    if fmt == "e4m3":
        byte = np.frexp(amax)[1] - 1 + 127 - 7
    else:
        mant, ex = np.frexp(amax / 6.0)
        byte = np.where(mant > 0.5, ex, ex - 1) + 127
    byte = np.clip(np.where(amax > 0, byte, 1), 1, 254)
    scaled = (w * np.exp2(127.0 - byte)[:, None, :]).reshape(k, n).astype(np.float32)
    by_word = np.ascontiguousarray(scaled.reshape(k // 512, 128, 4, n).transpose(0, 1, 3, 2))
    if fmt == "e4m3":
        words = by_word.astype(ml_dtypes.float8_e4m3fn).view(np.uint8)
    else:
        c = by_word.astype(ml_dtypes.float4_e2m1fn).view(np.uint8) & 0xF
        words = c[..., 0::2] | (c[..., 1::2] << 4)
    return np.ascontiguousarray(words), np.ascontiguousarray(byte.astype(np.uint8).reshape(k // 512, 16, n))


def unpack_weight(words, scales, fmt):
    g, p, n, _ = words.shape
    if fmt == "e4m3":
        vals = np.ascontiguousarray(words).view(ml_dtypes.float8_e4m3fn).astype(np.float64)
    else:
        nib = np.empty((g, p, n, 4), np.uint8)
        nib[..., 0::2] = words & 0xF
        nib[..., 1::2] = words >> 4
        vals = E2M1[nib]
    vals = vals * np.repeat(np.exp2(scales.astype(np.float64) - 127.0), 8, axis=1)[..., None]
    return vals.transpose(0, 1, 3, 2).reshape(g * 512, n)


B, T, C, QLR, H, R, KVL, VD = 4, 128, 2048, 1536, 16, 128, 512, 128
THETA = 10000.0
EPS = 1e-6
HALF = R // 2
FMT = "e4m3"


def rms_norm(v, w):
    return v / np.sqrt(np.mean(v * v, axis=-1, keepdims=True) + EPS) * w


def rope_cos_sin():
    inv = 1.0 / THETA ** (np.arange(HALF) / HALF)
    ang = np.arange(T)[:, None] * inv
    return np.cos(ang), np.sin(ang)


def apply_rot(v, cos, sin):
    vr, vi = v[..., 0::2], v[..., 1::2]
    c = cos[None, :, None, :]
    s = sin[None, :, None, :]
    return np.stack([vr * c - vi * s, vr * s + vi * c], axis=-1).reshape(v.shape)


def setup_inputs():
    s, t = mx_kscale(C), mx_kscale(KVL)
    x = bf(np.random.standard_normal((B, T, C)) * s)
    w_kva = np.random.standard_normal((KVL + R, C)) / np.sqrt(C) / s
    kva_norm_w = bf((1.0 + 0.1 * np.random.standard_normal(KVL)) * t)
    w_kvb = np.random.standard_normal((H * (R + VD), KVL)) / np.sqrt(KVL) / t
    w_kva_words, w_kva_scales = pack_weight(np.ascontiguousarray(w_kva.T), FMT)
    w_kvb_words, w_kvb_scales = pack_weight(np.ascontiguousarray(w_kvb.T), FMT)
    return {"x": x,
            "w_kva_words": w_kva_words,
            "w_kva_scales": w_kva_scales,
            "kva_norm_w": kva_norm_w,
            "w_kvb_words": w_kvb_words,
            "w_kvb_scales": w_kvb_scales}


def reference(x, w_kva_words, w_kva_scales, kva_norm_w, w_kvb_words, w_kvb_scales):
    kv_a = mxq(f64(x), 2, "e4m3") @ unpack_weight(w_kva_words, w_kva_scales, FMT)
    kv_c = rms_norm(kv_a[..., :KVL], f64(kva_norm_w))
    k_rope_raw = kv_a[..., KVL:]
    kv = (mxq(kv_c, 2, "e4m3") @ unpack_weight(w_kvb_words, w_kvb_scales, FMT)).reshape(B, T, H, R + VD)
    k_content, v = kv[..., :R], kv[..., R:]
    k_rope = np.broadcast_to(k_rope_raw[:, :, None, :], (B, T, H, R))
    cos, sin = rope_cos_sin()
    k = np.concatenate([k_content, apply_rot(k_rope, cos, sin)], axis=-1)
    return k, v

@@ -1,0 +1,280 @@
+import math
+from contextlib import ExitStack
+
+import concourse.masks as masks
+import concourse.mybir as mybir
+
+F32 = mybir.dt.float32
+BF16 = mybir.dt.bfloat16
+I32 = mybir.dt.int32
+U32 = mybir.dt.uint32
+U8 = mybir.dt.uint8
+FP8X4 = mybir.dt.float8_e4m3fn_x4
+ALU = mybir.AluOpType
+ACT = mybir.ActivationFunctionType
+
+P = 128
+PACK = 4
+K_PASS = P * PACK
+TILES = 4
+C = 2048
+X_PASSES = C // K_PASS
+LATENT = 512
+ROPE = 128
+HALF = ROPE // 2
+A_COLS = LATENT + ROPE
+HEADS = 16
+HEAD_DIM = 128
+KV_COLS = HEADS * 2 * HEAD_DIM
+BANK = 512
+KV_BANKS = KV_COLS // BANK
+HEADS_PER_BANK = BANK // (2 * HEAD_DIM)
+PLANES = 4
+PLANE_COLS = KV_COLS // PLANES
+HEADS_PER_STORE = 8
+THETA = 10000.0
+EPS = 1e-6
+ROUND_MAGIC = 1.5 * 2.0**23
+
+FLOPS = 2 * TILES * P * (C * A_COLS + LATENT * KV_COLS)
+
+
+def tile_multiheadlatentattention_pb_kernel(
+    tc, x, w_kva_words, w_kva_scales, kva_norm_w, w_kvb_words, w_kvb_scales, out_0, out_1
+):
+    nc = tc.nc
+    with ExitStack() as ctx:
+        keep = ctx.enter_context(tc.tile_pool(name="keep", bufs=1))
+        work = ctx.enter_context(tc.tile_pool(name="work", bufs=2))
+        wide_psum = ctx.enter_context(tc.psum_pool(name="wide_psum", bufs=6))
+        narrow_psum = ctx.enter_context(tc.psum_pool(name="narrow_psum", bufs=2))
+        ctx.enter_context(tc.manual_schedule())
+
+        x_sb = [keep.tile([P, C], BF16, name="x_sb%d" % i) for i in range(TILES)]
+        w1_words = keep.tile([P, X_PASSES, A_COLS], U32, align_bytes=64)
+        w2_words = keep.tile([P, KV_COLS], U32, align_bytes=64)
+        w1_planes = keep.tile([P, A_COLS], U8, align_bytes=64)
+        w2_planes = keep.tile([P, PLANE_COLS], U8, align_bytes=64)
+        x_grouped = [
+            keep.tile([P, X_PASSES, P, PACK], BF16, name="x_grouped%d" % i, align_bytes=64)
+            for i in range(TILES)
+        ]
+        x_codes = [keep.tile([P, X_PASSES * P], U32, name="x_codes%d" % i, align_bytes=64) for i in range(TILES)]
+        x_scales = [keep.tile([P, X_PASSES * P], U8, name="x_scales%d" % i, align_bytes=64) for i in range(TILES)]
+        c_codes = [keep.tile([P, P], U32, name="c_codes%d" % i, align_bytes=64) for i in range(TILES)]
+        c_scales = [keep.tile([P, P], U8, name="c_scales%d" % i, align_bytes=64) for i in range(TILES)]
+        k_sb = [keep.tile([P, HEADS, 2 * HEAD_DIM], F32, name="k_sb%d" % i) for i in range(TILES)]
+        v_sb = [keep.tile([P, HEADS, HEAD_DIM], F32, name="v_sb%d" % i) for i in range(TILES)]
+
+        nc.vector.memset(w1_planes[:].bitcast(I32), 0)
+        nc.vector.memset(w2_planes[:].bitcast(I32), 0)
+
+        w1_scale_rows = w_kva_scales.bitcast(I32)
+        w2_scale_rows = w_kvb_scales[0].bitcast(I32)
+        w1_word_rows = w_kva_words.rearrange("g p n t -> g p (n t)").bitcast(I32)
+        w2_word_rows = w_kvb_words[0].rearrange("p n t -> p (n t)").bitcast(I32)
+
+        nc.sync.dma_start(out=x_sb[0][:], in_=x[0])
+        for quadrant in range(4):
+            nc.sync.dma_start(
+                out=w1_planes[32 * quadrant : 32 * quadrant + 16, :].bitcast(I32),
+                in_=w1_scale_rows[:, 4 * quadrant : 4 * quadrant + 4, :],
+            )
+        for g in range(0, X_PASSES, 2):
+            nc.sync.dma_start(
+                out=w1_words[:, g : g + 2, :].bitcast(I32), in_=w1_word_rows[g : g + 2].rearrange("g p w -> p g w")
+            )
+        nc.sync.dma_start(out=x_sb[1][:], in_=x[1])
+        for quadrant in range(4):
+            nc.sync.dma_start(
+                out=w2_planes[32 * quadrant : 32 * quadrant + 16, :].bitcast(I32),
+                in_=w2_scale_rows[4 * quadrant : 4 * quadrant + 4, :].rearrange("r (j c) -> j r c", j=PLANES),
+            )
+        for j in range(PLANES):
+            cols = slice(PLANE_COLS * j, PLANE_COLS * (j + 1))
+            nc.sync.dma_start(out=w2_words[:, cols].bitcast(I32), in_=w2_word_rows[:, cols])
+        nc.sync.dma_start(out=x_sb[2][:], in_=x[2])
+        nc.sync.dma_start(out=x_sb[3][:], in_=x[3])
+
+        gain_row = keep.tile([P, LATENT], BF16)
+        nc.vector.memset(gain_row[:].bitcast(I32), 0)
+        nc.scalar.dma_start(out=gain_row[0:1, :], in_=kva_norm_w.unsqueeze(0))
+        position = keep.tile([P, 1], I32)
+        nc.gpsimd.iota(position[:], pattern=[[0, 1]], base=0, channel_multiplier=1)
+        ident_f32 = keep.tile([P, P], F32)
+        masks.make_identity(nc, ident_f32[:])
+        ones = keep.tile([P, P], BF16)
+        nc.gpsimd.memset(ones[:], 1.0)
+        ident_bf16 = keep.tile([P, P], BF16)
+        masks.make_identity(nc, ident_bf16[:])
+
+        turns = keep.tile([P, 2, HALF], F32)
+        nc.vector.tensor_scalar_mul(out=turns[:, 1, 0:1], in0=position[:], scalar1=1.0 / (2.0 * math.pi))
+        for doubling in range(6):
+            width = 2**doubling
+            nc.vector.tensor_scalar_mul(
+                out=turns[:, 1, width : 2 * width], in0=turns[:, 1, 0:width], scalar1=THETA ** (-width / HALF)
+            )
+        nc.vector.tensor_scalar_add(out=turns[:, 0, :], in0=turns[:, 1, :], scalar1=0.25)
+        whole_turns = keep.tile([P, 2, HALF], F32)
+        nc.vector.tensor_scalar(
+            out=whole_turns[:], in0=turns[:], scalar1=ROUND_MAGIC, scalar2=ROUND_MAGIC, op0=ALU.add, op1=ALU.subtract
+        )
+        part_turns = keep.tile([P, 2, HALF], F32)
+        nc.vector.tensor_sub(out=part_turns[:], in0=turns[:], in1=whole_turns[:])
+        table = keep.tile([P, 4, HALF], F32)
+        nc.scalar.activation(out=table[:, 0:2, :], in_=part_turns[:], func=ACT.Sin, scale=2.0 * math.pi)
+        nc.vector.tensor_scalar_mul(out=table[:, 2, :], in0=table[:, 1, :], scalar1=-1.0)
+        nc.vector.tensor_copy(out=table[:, 3, :], in_=table[:, 0, :])
+        warm = keep.tile([P, 1], F32)
+        nc.scalar.activation(out=warm[:], in_=table[:, 0, 0:1], func=ACT.Abs_reciprocal_sqrt, scale=0.0, bias=1.0)
+
+        gain = keep.tile([P, PACK, P], F32)
+
+        def spread_gain():
+            gain_psum = wide_psum.tile([P, BANK], F32, tag="wide")
+            nc.tensor.matmul(out=gain_psum[:], lhsT=ones[:], rhs=gain_row[:], start=True, stop=True)
+            nc.vector.tensor_copy(out=gain[:], in_=gain_psum[:].rearrange("p (q t) -> p t q", t=PACK))
+
+        def copy_out_of_psum(piece, out, in_):
+            if piece % 2 == 0:
+                nc.vector.tensor_copy(out=out, in_=in_)
+            else:
+                nc.scalar.copy(out=out, in_=in_)
+
+        def transpose_x(i):
+            pairs = x_sb[i][:].bitcast(F32)
+            x_t = []
+            for half in range(2):
+                x_t_half = wide_psum.tile([P, 2, 2, P], F32, tag="wide")
+                for g2 in range(2):
+                    g = 2 * half + g2
+                    for u in range(2):
+                        nc.tensor.transpose(
+                            x_t_half[:, g2, u, :], pairs[:, 256 * g + u : 256 * (g + 1) : 2], ident_f32[:]
+                        )
+                x_t.append(x_t_half)
+            return x_t
+
+        def quantise_x(i, x_t):
+            for half in range(2):
+                copy_out_of_psum(
+                    half,
+                    out=x_grouped[i][:, 2 * half : 2 * half + 2, :, :].bitcast(F32),
+                    in_=x_t[half][:].rearrange("p g u k -> p g k u"),
+                )
+            for half in range(2):
+                cols = slice(2 * P * half, 2 * P * (half + 1))
+                nc.vector.quantize_mx(
+                    out=x_codes[i][:, cols].bitcast(FP8X4),
+                    scales=x_scales[i][:, cols],
+                    in_=x_grouped[i][:, 2 * half : 2 * half + 2, :, :].rearrange("p g k t -> p (g k t)"),
+                )
+
+        def first_matmul(i):
+            latent = wide_psum.tile([P, LATENT], F32, tag="wide")
+            raw_rope = narrow_psum.tile([P, ROPE], F32, tag="narrow")
+            for g in range(X_PASSES):
+                tokens = slice(P * g, P * (g + 1))
+                for acc, cols in ((latent, slice(0, LATENT)), (raw_rope, slice(LATENT, A_COLS))):
+                    nc.tensor.matmul_mx(
+                        out=acc[:],
+                        lhsT=x_codes[i][:, tokens].bitcast(FP8X4),
+                        lhsT_scale=x_scales[i][:, tokens],
+                        rhs=w1_words[:, g, cols].bitcast(FP8X4),
+                        rhs_scale=w1_planes[4 * g : P, cols],
+                        start=(g == 0),
+                        stop=(g == X_PASSES - 1),
+                    )
+            return latent, raw_rope
+
+        def norm_and_rotate(i, latent, raw_rope):
+            by_parity = raw_rope[:].rearrange("p (j e) -> p e j", e=2)
+            from_even = work.tile([P, 2, HALF], F32)
+            nc.vector.tensor_tensor(
+                out=from_even[:], in0=by_parity[:, 0:1, :].to_broadcast([P, 2, HALF]), in1=table[:, 0:2, :], op=ALU.mult
+            )
+            from_odd = work.tile([P, 2, HALF], F32)
+            nc.vector.tensor_tensor(
+                out=from_odd[:], in0=by_parity[:, 1:2, :].to_broadcast([P, 2, HALF]), in1=table[:, 2:4, :], op=ALU.mult
+            )
+            rotated = work.tile([P, HALF, 2], F32)
+            nc.vector.tensor_tensor(
+                out=rotated[:],
+                in0=from_even[:].rearrange("p e j -> p j e"),
+                in1=from_odd[:].rearrange("p e j -> p j e"),
+                op=ALU.add,
+            )
+
+            squares = work.tile([P, LATENT], BF16)
+            sum_squares = work.tile([P, 1], F32)
+            nc.scalar.activation(out=squares[:], in_=latent[:], func=ACT.Square, accum_out=sum_squares[:])
+            inv_rms = work.tile([P, 1], F32)
+            nc.scalar.activation(
+                out=inv_rms[:], in_=sum_squares[:], func=ACT.Abs_reciprocal_sqrt, scale=1.0 / LATENT, bias=EPS
+            )
+            c_sb = work.tile([P, PACK, P], BF16)
+            nc.vector.scalar_tensor_tensor(
+                out=c_sb[:],
+                in0=latent[:].rearrange("p (q t) -> p t q", t=PACK),
+                scalar=inv_rms[:],
+                in1=gain[:],
+                op0=ALU.mult,
+                op1=ALU.mult,
+            )
+            nc.scalar.copy(
+                out=k_sb[i][:, :, HEAD_DIM:],
+                in_=rotated[:].rearrange("p j e -> p (j e)").unsqueeze(1).to_broadcast([P, HEADS, ROPE]),
+            )
+            return c_sb
+
+        def quantise_c(i, c_sb):
+            c_t = narrow_psum.tile([P, PACK, P], BF16, tag="narrow")
+            for t in range(PACK):
+                nc.tensor.transpose(c_t[:, t, :], c_sb[:, t, :], ident_bf16[:])
+            c_grouped = work.tile([P, P, PACK], BF16, align_bytes=64)
+            nc.vector.tensor_copy(out=c_grouped[:], in_=c_t[:].rearrange("p t k -> p k t"))
+            nc.vector.quantize_mx(
+                out=c_codes[i][:].bitcast(FP8X4),
+                scales=c_scales[i][:],
+                in_=c_grouped[:].rearrange("p k t -> p (k t)"),
+            )
+
+        def second_matmul(i, first_head):
+            stored = slice(first_head, first_head + HEADS_PER_STORE)
+            first_bank = first_head // HEADS_PER_BANK
+            for bank in range(first_bank, first_bank + HEADS_PER_STORE // HEADS_PER_BANK):
+                kv = wide_psum.tile([P, HEADS_PER_BANK, 2, HEAD_DIM], F32, tag="wide")
+                plane = (BANK * bank) // PLANE_COLS
+                plane_cols = slice((BANK * bank) % PLANE_COLS, (BANK * bank) % PLANE_COLS + BANK)
+                nc.tensor.matmul_mx(
+                    out=kv[:].rearrange("p h s d -> p (h s d)"),
+                    lhsT=c_codes[i][:].bitcast(FP8X4),
+                    lhsT_scale=c_scales[i][:],
+                    rhs=w2_words[:, BANK * bank : BANK * (bank + 1)].bitcast(FP8X4),
+                    rhs_scale=w2_planes[4 * plane : P, plane_cols],
+                    start=True,
+                    stop=True,
+                )
+                heads = slice(HEADS_PER_BANK * bank, HEADS_PER_BANK * (bank + 1))
+                copy_out_of_psum(bank, out=k_sb[i][:, heads, 0:HEAD_DIM], in_=kv[:, :, 0, :])
+                copy_out_of_psum(bank, out=v_sb[i][:, heads, :], in_=kv[:, :, 1, :])
+            nc.sync.dma_start(out=out_0[i, :, stored, :], in_=k_sb[i][:, stored, :])
+            nc.sync.dma_start(out=out_1[i, :, stored, :], in_=v_sb[i][:, stored, :])
+
+        quantise_x(0, transpose_x(0))
+        spread_gain()
+        latent, raw_rope = first_matmul(0)
+        c_sb = norm_and_rotate(0, latent, raw_rope)
+        for i in range(TILES):
+            more = i + 1 < TILES
+            if more:
+                x_t = transpose_x(i + 1)
+            quantise_c(i, c_sb)
+            if more:
+                quantise_x(i + 1, x_t)
+            second_matmul(i, 0)
+            if more:
+                latent, raw_rope = first_matmul(i + 1)
+                c_sb = norm_and_rotate(i + 1, latent, raw_rope)
+            second_matmul(i, HEADS_PER_STORE)

@@ -222,10 +222,15 @@ def tile_multiheadlatentattention_pb_kernel(
                 op0=ALU.mult,
                 op1=ALU.mult,
             )
-            nc.scalar.copy(
-                out=k_sb[i][:, :, HEAD_DIM:],
-                in_=rotated[:].rearrange("p j e -> p (j e)").unsqueeze(1).to_broadcast([P, HEADS, ROPE]),
-            )
+            for first_head in range(0, HEADS, HEADS_PER_STORE):
+                nc.gpsimd.tensor_scalar(
+                    out=k_sb[i][:, first_head : first_head + HEADS_PER_STORE, HEAD_DIM:],
+                    in0=rotated[:].rearrange("p j e -> p (j e)").unsqueeze(1).to_broadcast([P, HEADS_PER_STORE, ROPE]),
+                    scalar1=1.0,
+                    scalar2=0.0,
+                    op0=ALU.mult,
+                    op1=ALU.add,
+                )
             return c_sb
 
         def quantise_c(i, c_sb):

@@ -46,7 +46,8 @@ def tile_multiheadlatentattention_pb_kernel(
     with ExitStack() as ctx:
         keep = ctx.enter_context(tc.tile_pool(name="keep", bufs=1))
         work = ctx.enter_context(tc.tile_pool(name="work", bufs=2))
-        wide_psum = ctx.enter_context(tc.psum_pool(name="wide_psum", bufs=6))
+        wide_psum = ctx.enter_context(tc.psum_pool(name="wide_psum", bufs=5))
+        latent_psum = ctx.enter_context(tc.psum_pool(name="latent_psum", bufs=1))
         narrow_psum = ctx.enter_context(tc.psum_pool(name="narrow_psum", bufs=2))
         ctx.enter_context(tc.manual_schedule())
 
@@ -74,7 +75,14 @@ def tile_multiheadlatentattention_pb_kernel(
         w1_word_rows = w_kva_words.rearrange("g p n t -> g p (n t)").bitcast(I32)
         w2_word_rows = w_kvb_words[0].rearrange("p n t -> p (n t)").bitcast(I32)
 
-        nc.sync.dma_start(out=x_sb[0][:], in_=x[0])
+        def load_x(i):
+            nc.sync.dma_start(out=x_sb[i][:], in_=x[i])
+
+        def load_w2_words(j):
+            cols = slice(PLANE_COLS * j, PLANE_COLS * (j + 1))
+            nc.sync.dma_start(out=w2_words[:, cols].bitcast(I32), in_=w2_word_rows[:, cols])
+
+        load_x(0)
         for quadrant in range(4):
             nc.sync.dma_start(
                 out=w1_planes[32 * quadrant : 32 * quadrant + 16, :].bitcast(I32),
@@ -84,17 +92,18 @@ def tile_multiheadlatentattention_pb_kernel(
             nc.sync.dma_start(
                 out=w1_words[:, g : g + 2, :].bitcast(I32), in_=w1_word_rows[g : g + 2].rearrange("g p w -> p g w")
             )
-        nc.sync.dma_start(out=x_sb[1][:], in_=x[1])
+        load_x(1)
         for quadrant in range(4):
             nc.sync.dma_start(
                 out=w2_planes[32 * quadrant : 32 * quadrant + 16, :].bitcast(I32),
                 in_=w2_scale_rows[4 * quadrant : 4 * quadrant + 4, :].rearrange("r (j c) -> j r c", j=PLANES),
             )
-        for j in range(PLANES):
-            cols = slice(PLANE_COLS * j, PLANE_COLS * (j + 1))
-            nc.sync.dma_start(out=w2_words[:, cols].bitcast(I32), in_=w2_word_rows[:, cols])
-        nc.sync.dma_start(out=x_sb[2][:], in_=x[2])
-        nc.sync.dma_start(out=x_sb[3][:], in_=x[3])
+        load_w2_words(0)
+        load_w2_words(1)
+        load_x(2)
+        load_w2_words(2)
+        load_w2_words(3)
+        load_x(3)
 
         gain_row = keep.tile([P, LATENT], BF16)
         nc.vector.memset(gain_row[:].bitcast(I32), 0)
@@ -136,8 +145,8 @@ def tile_multiheadlatentattention_pb_kernel(
             nc.tensor.matmul(out=gain_psum[:], lhsT=ones[:], rhs=gain_row[:], start=True, stop=True)
             nc.vector.tensor_copy(out=gain[:], in_=gain_psum[:].rearrange("p (q t) -> p t q", t=PACK))
 
-        def copy_out_of_psum(piece, out, in_):
-            if piece % 2 == 0:
+        def copy_out_of_psum(on_vector, out, in_):
+            if on_vector:
                 nc.vector.tensor_copy(out=out, in_=in_)
             else:
                 nc.scalar.copy(out=out, in_=in_)
@@ -156,13 +165,15 @@ def tile_multiheadlatentattention_pb_kernel(
                 x_t.append(x_t_half)
             return x_t
 
-        def quantise_x(i, x_t):
+        def group_x(i, x_t):
             for half in range(2):
                 copy_out_of_psum(
-                    half,
+                    half == 0,
                     out=x_grouped[i][:, 2 * half : 2 * half + 2, :, :].bitcast(F32),
                     in_=x_t[half][:].rearrange("p g u k -> p g k u"),
                 )
+
+        def quantise_x(i):
             for half in range(2):
                 cols = slice(2 * P * half, 2 * P * (half + 1))
                 nc.vector.quantize_mx(
@@ -172,7 +183,7 @@ def tile_multiheadlatentattention_pb_kernel(
                 )
 
         def first_matmul(i):
-            latent = wide_psum.tile([P, LATENT], F32, tag="wide")
+            latent = latent_psum.tile([P, LATENT], F32)
             raw_rope = narrow_psum.tile([P, ROPE], F32, tag="narrow")
             for g in range(X_PASSES):
                 tokens = slice(P * g, P * (g + 1))
@@ -188,7 +199,7 @@ def tile_multiheadlatentattention_pb_kernel(
                     )
             return latent, raw_rope
 
-        def norm_and_rotate(i, latent, raw_rope):
+        def rotate(raw_rope):
             by_parity = raw_rope[:].rearrange("p (j e) -> p e j", e=2)
             from_even = work.tile([P, 2, HALF], F32)
             nc.vector.tensor_tensor(
@@ -205,23 +216,9 @@ def tile_multiheadlatentattention_pb_kernel(
                 in1=from_odd[:].rearrange("p e j -> p j e"),
                 op=ALU.add,
             )
+            return rotated
 
-            squares = work.tile([P, LATENT], BF16)
-            sum_squares = work.tile([P, 1], F32)
-            nc.scalar.activation(out=squares[:], in_=latent[:], func=ACT.Square, accum_out=sum_squares[:])
-            inv_rms = work.tile([P, 1], F32)
-            nc.scalar.activation(
-                out=inv_rms[:], in_=sum_squares[:], func=ACT.Abs_reciprocal_sqrt, scale=1.0 / LATENT, bias=EPS
-            )
-            c_sb = work.tile([P, PACK, P], BF16)
-            nc.vector.scalar_tensor_tensor(
-                out=c_sb[:],
-                in0=latent[:].rearrange("p (q t) -> p t q", t=PACK),
-                scalar=inv_rms[:],
-                in1=gain[:],
-                op0=ALU.mult,
-                op1=ALU.mult,
-            )
+        def repeat_rotated(i, rotated):
             for first_head in range(0, HEADS, HEADS_PER_STORE):
                 nc.gpsimd.tensor_scalar(
                     out=k_sb[i][:, first_head : first_head + HEADS_PER_STORE, HEAD_DIM:],
@@ -231,6 +228,27 @@ def tile_multiheadlatentattention_pb_kernel(
                     op0=ALU.mult,
                     op1=ALU.add,
                 )
+
+        def inverse_rms(latent):
+            squares = work.tile([P, LATENT], BF16)
+            sum_squares = work.tile([P, 1], F32)
+            nc.scalar.activation(out=squares[:], in_=latent[:], func=ACT.Square, accum_out=sum_squares[:])
+            inv_rms = work.tile([P, 1], F32)
+            nc.scalar.activation(
+                out=inv_rms[:], in_=sum_squares[:], func=ACT.Abs_reciprocal_sqrt, scale=1.0 / LATENT, bias=EPS
+            )
+            return inv_rms
+
+        def scale_c(latent, inv_rms):
+            c_sb = work.tile([P, PACK, P], BF16)
+            nc.vector.scalar_tensor_tensor(
+                out=c_sb[:],
+                in0=latent[:].rearrange("p (q t) -> p t q", t=PACK),
+                scalar=inv_rms[:],
+                in1=gain[:],
+                op0=ALU.mult,
+                op1=ALU.mult,
+            )
             return c_sb
 
         def quantise_c(i, c_sb):
@@ -262,24 +280,39 @@ def tile_multiheadlatentattention_pb_kernel(
                     stop=True,
                 )
                 heads = slice(HEADS_PER_BANK * bank, HEADS_PER_BANK * (bank + 1))
-                copy_out_of_psum(bank, out=k_sb[i][:, heads, 0:HEAD_DIM], in_=kv[:, :, 0, :])
-                copy_out_of_psum(bank, out=v_sb[i][:, heads, :], in_=kv[:, :, 1, :])
-            nc.sync.dma_start(out=out_0[i, :, stored, :], in_=k_sb[i][:, stored, :])
-            nc.sync.dma_start(out=out_1[i, :, stored, :], in_=v_sb[i][:, stored, :])
+                on_vector = bank % 3 == 0
+                copy_out_of_psum(on_vector, out=k_sb[i][:, heads, 0:HEAD_DIM], in_=kv[:, :, 0, :])
+                copy_out_of_psum(on_vector, out=v_sb[i][:, heads, :], in_=kv[:, :, 1, :])
+            nc.sync.dma_start(
+                out=out_0[i, :, stored, :].rearrange("t h d -> t (h d)"),
+                in_=k_sb[i][:, stored, :].rearrange("p h d -> p (h d)"),
+            )
+            nc.sync.dma_start(
+                out=out_1[i, :, stored, :].rearrange("t h d -> t (h d)"),
+                in_=v_sb[i][:, stored, :].rearrange("p h d -> p (h d)"),
+            )
 
-        quantise_x(0, transpose_x(0))
+        group_x(0, transpose_x(0))
+        quantise_x(0)
         spread_gain()
         latent, raw_rope = first_matmul(0)
-        c_sb = norm_and_rotate(0, latent, raw_rope)
+        rotated = rotate(raw_rope)
+        inv_rms = inverse_rms(latent)
+        group_x(1, transpose_x(1))
+        c_sb = scale_c(latent, inv_rms)
+        repeat_rotated(0, rotated)
+        quantise_x(1)
         for i in range(TILES):
-            more = i + 1 < TILES
-            if more:
-                x_t = transpose_x(i + 1)
             quantise_c(i, c_sb)
-            if more:
-                quantise_x(i + 1, x_t)
-            second_matmul(i, 0)
-            if more:
+            if i + 1 < TILES:
                 latent, raw_rope = first_matmul(i + 1)
-                c_sb = norm_and_rotate(i + 1, latent, raw_rope)
+                rotated = rotate(raw_rope)
+                inv_rms = inverse_rms(latent)
+            second_matmul(i, 0)
+            if i + 1 < TILES:
+                c_sb = scale_c(latent, inv_rms)
+                repeat_rotated(i + 1, rotated)
+            if i + 2 < TILES:
+                group_x(i + 2, transpose_x(i + 2))
+                quantise_x(i + 2)
             second_matmul(i, HEADS_PER_STORE)

@@ -31,7 +31,8 @@ KV_BANKS = KV_COLS // BANK
 HEADS_PER_BANK = BANK // (2 * HEAD_DIM)
 PLANES = 4
 PLANE_COLS = KV_COLS // PLANES
-HEADS_PER_STORE = 8
+HALF_HEADS = HEADS // 2
+FIRST_STORE_HEADS = 4
 THETA = 10000.0
 EPS = 1e-6
 ROUND_MAGIC = 1.5 * 2.0**23
@@ -78,11 +79,12 @@ def tile_multiheadlatentattention_pb_kernel(
         def load_x(i):
             nc.sync.dma_start(out=x_sb[i][:], in_=x[i])
 
-        def load_w2_words(j):
-            cols = slice(PLANE_COLS * j, PLANE_COLS * (j + 1))
+        def load_w2_words(half):
+            cols = slice(KV_COLS // 2 * half, KV_COLS // 2 * (half + 1))
             nc.sync.dma_start(out=w2_words[:, cols].bitcast(I32), in_=w2_word_rows[:, cols])
 
-        load_x(0)
+        nc.sync.dma_start(out=x_sb[0][:, 0 : C // 2], in_=x[0, :, 0 : C // 2])
+        nc.sync.dma_start(out=x_sb[0][:, C // 2 : C], in_=x[0, :, C // 2 : C])
         for quadrant in range(4):
             nc.sync.dma_start(
                 out=w1_planes[32 * quadrant : 32 * quadrant + 16, :].bitcast(I32),
@@ -99,10 +101,8 @@ def tile_multiheadlatentattention_pb_kernel(
                 in_=w2_scale_rows[4 * quadrant : 4 * quadrant + 4, :].rearrange("r (j c) -> j r c", j=PLANES),
             )
         load_w2_words(0)
-        load_w2_words(1)
         load_x(2)
-        load_w2_words(2)
-        load_w2_words(3)
+        load_w2_words(1)
         load_x(3)
 
         gain_row = keep.tile([P, LATENT], BF16)
@@ -185,9 +185,9 @@ def tile_multiheadlatentattention_pb_kernel(
         def first_matmul(i):
             latent = latent_psum.tile([P, LATENT], F32)
             raw_rope = narrow_psum.tile([P, ROPE], F32, tag="narrow")
-            for g in range(X_PASSES):
-                tokens = slice(P * g, P * (g + 1))
-                for acc, cols in ((latent, slice(0, LATENT)), (raw_rope, slice(LATENT, A_COLS))):
+            for acc, cols in ((latent, slice(0, LATENT)), (raw_rope, slice(LATENT, A_COLS))):
+                for g in range(X_PASSES):
+                    tokens = slice(P * g, P * (g + 1))
                     nc.tensor.matmul_mx(
                         out=acc[:],
                         lhsT=x_codes[i][:, tokens].bitcast(FP8X4),
@@ -219,10 +219,10 @@ def tile_multiheadlatentattention_pb_kernel(
             return rotated
 
         def repeat_rotated(i, rotated):
-            for first_head in range(0, HEADS, HEADS_PER_STORE):
+            for first_head in range(0, HEADS, HALF_HEADS):
                 nc.gpsimd.tensor_scalar(
-                    out=k_sb[i][:, first_head : first_head + HEADS_PER_STORE, HEAD_DIM:],
-                    in0=rotated[:].rearrange("p j e -> p (j e)").unsqueeze(1).to_broadcast([P, HEADS_PER_STORE, ROPE]),
+                    out=k_sb[i][:, first_head : first_head + HALF_HEADS, HEAD_DIM:],
+                    in0=rotated[:].rearrange("p j e -> p (j e)").unsqueeze(1).to_broadcast([P, HALF_HEADS, ROPE]),
                     scalar1=1.0,
                     scalar2=0.0,
                     op0=ALU.mult,
@@ -263,10 +263,10 @@ def tile_multiheadlatentattention_pb_kernel(
                 in_=c_grouped[:].rearrange("p k t -> p (k t)"),
             )
 
-        def second_matmul(i, first_head):
-            stored = slice(first_head, first_head + HEADS_PER_STORE)
+        def second_matmul(i, first_head, heads_stored):
+            stored = slice(first_head, first_head + heads_stored)
             first_bank = first_head // HEADS_PER_BANK
-            for bank in range(first_bank, first_bank + HEADS_PER_STORE // HEADS_PER_BANK):
+            for bank in range(first_bank, first_bank + heads_stored // HEADS_PER_BANK):
                 kv = wide_psum.tile([P, HEADS_PER_BANK, 2, HEAD_DIM], F32, tag="wide")
                 plane = (BANK * bank) // PLANE_COLS
                 plane_cols = slice((BANK * bank) % PLANE_COLS, (BANK * bank) % PLANE_COLS + BANK)
@@ -292,6 +292,11 @@ def tile_multiheadlatentattention_pb_kernel(
                 in_=v_sb[i][:, stored, :].rearrange("p h d -> p (h d)"),
             )
 
+        def second_matmul_half(i, half):
+            heads_stored = FIRST_STORE_HEADS if i == 0 else HALF_HEADS
+            for first_head in range(HALF_HEADS * half, HALF_HEADS * (half + 1), heads_stored):
+                second_matmul(i, first_head, heads_stored)
+
         group_x(0, transpose_x(0))
         quantise_x(0)
         spread_gain()
@@ -308,11 +313,11 @@ def tile_multiheadlatentattention_pb_kernel(
                 latent, raw_rope = first_matmul(i + 1)
                 rotated = rotate(raw_rope)
                 inv_rms = inverse_rms(latent)
-            second_matmul(i, 0)
+            second_matmul_half(i, 0)
             if i + 1 < TILES:
                 c_sb = scale_c(latent, inv_rms)
                 repeat_rotated(i + 1, rotated)
             if i + 2 < TILES:
                 group_x(i + 2, transpose_x(i + 2))
                 quantise_x(i + 2)
-            second_matmul(i, HEADS_PER_STORE)
+            second_matmul_half(i, 1)

@@ -32,7 +32,7 @@ HEADS_PER_BANK = BANK // (2 * HEAD_DIM)
 PLANES = 4
 PLANE_COLS = KV_COLS // PLANES
 HALF_HEADS = HEADS // 2
-FIRST_STORE_HEADS = 4
+TILES_STORED_BY_HALVES = 2
 THETA = 10000.0
 EPS = 1e-6
 ROUND_MAGIC = 1.5 * 2.0**23
@@ -83,8 +83,7 @@ def tile_multiheadlatentattention_pb_kernel(
             cols = slice(KV_COLS // 2 * half, KV_COLS // 2 * (half + 1))
             nc.sync.dma_start(out=w2_words[:, cols].bitcast(I32), in_=w2_word_rows[:, cols])
 
-        nc.sync.dma_start(out=x_sb[0][:, 0 : C // 2], in_=x[0, :, 0 : C // 2])
-        nc.sync.dma_start(out=x_sb[0][:, C // 2 : C], in_=x[0, :, C // 2 : C])
+        load_x(0)
         for quadrant in range(4):
             nc.sync.dma_start(
                 out=w1_planes[32 * quadrant : 32 * quadrant + 16, :].bitcast(I32),
@@ -263,10 +262,8 @@ def tile_multiheadlatentattention_pb_kernel(
                 in_=c_grouped[:].rearrange("p k t -> p (k t)"),
             )
 
-        def second_matmul(i, first_head, heads_stored):
-            stored = slice(first_head, first_head + heads_stored)
-            first_bank = first_head // HEADS_PER_BANK
-            for bank in range(first_bank, first_bank + heads_stored // HEADS_PER_BANK):
+        def second_matmul(i, half):
+            for bank in range(KV_BANKS // 2 * half, KV_BANKS // 2 * (half + 1)):
                 kv = wide_psum.tile([P, HEADS_PER_BANK, 2, HEAD_DIM], F32, tag="wide")
                 plane = (BANK * bank) // PLANE_COLS
                 plane_cols = slice((BANK * bank) % PLANE_COLS, (BANK * bank) % PLANE_COLS + BANK)
@@ -283,6 +280,9 @@ def tile_multiheadlatentattention_pb_kernel(
                 on_vector = bank % 3 == 0
                 copy_out_of_psum(on_vector, out=k_sb[i][:, heads, 0:HEAD_DIM], in_=kv[:, :, 0, :])
                 copy_out_of_psum(on_vector, out=v_sb[i][:, heads, :], in_=kv[:, :, 1, :])
+
+        def store(i, first_head, heads_stored):
+            stored = slice(first_head, first_head + heads_stored)
             nc.sync.dma_start(
                 out=out_0[i, :, stored, :].rearrange("t h d -> t (h d)"),
                 in_=k_sb[i][:, stored, :].rearrange("p h d -> p (h d)"),
@@ -291,11 +291,6 @@ def tile_multiheadlatentattention_pb_kernel(
                 out=out_1[i, :, stored, :].rearrange("t h d -> t (h d)"),
                 in_=v_sb[i][:, stored, :].rearrange("p h d -> p (h d)"),
             )
-
-        def second_matmul_half(i, half):
-            heads_stored = FIRST_STORE_HEADS if i == 0 else HALF_HEADS
-            for first_head in range(HALF_HEADS * half, HALF_HEADS * (half + 1), heads_stored):
-                second_matmul(i, first_head, heads_stored)
 
         group_x(0, transpose_x(0))
         quantise_x(0)
@@ -313,11 +308,17 @@ def tile_multiheadlatentattention_pb_kernel(
                 latent, raw_rope = first_matmul(i + 1)
                 rotated = rotate(raw_rope)
                 inv_rms = inverse_rms(latent)
-            second_matmul_half(i, 0)
+            second_matmul(i, 0)
+            if i < TILES_STORED_BY_HALVES:
+                store(i, 0, HALF_HEADS)
             if i + 1 < TILES:
                 c_sb = scale_c(latent, inv_rms)
                 repeat_rotated(i + 1, rotated)
             if i + 2 < TILES:
                 group_x(i + 2, transpose_x(i + 2))
                 quantise_x(i + 2)
-            second_matmul_half(i, 1)
+            second_matmul(i, 1)
+            if i < TILES_STORED_BY_HALVES:
+                store(i, HALF_HEADS, HALF_HEADS)
+            else:
+                store(i, 0, HEADS)

@@ -32,6 +32,7 @@ HEADS_PER_BANK = BANK // (2 * HEAD_DIM)
 PLANES = 4
 PLANE_COLS = KV_COLS // PLANES
 HALF_HEADS = HEADS // 2
+VECTOR_BANKS = (0, 3, 6)
 TILES_STORED_BY_HALVES = 2
 THETA = 10000.0
 EPS = 1e-6
@@ -84,6 +85,7 @@ def tile_multiheadlatentattention_pb_kernel(
             nc.sync.dma_start(out=w2_words[:, cols].bitcast(I32), in_=w2_word_rows[:, cols])
 
         load_x(0)
+        load_x(1)
         for quadrant in range(4):
             nc.sync.dma_start(
                 out=w1_planes[32 * quadrant : 32 * quadrant + 16, :].bitcast(I32),
@@ -93,14 +95,13 @@ def tile_multiheadlatentattention_pb_kernel(
             nc.sync.dma_start(
                 out=w1_words[:, g : g + 2, :].bitcast(I32), in_=w1_word_rows[g : g + 2].rearrange("g p w -> p g w")
             )
-        load_x(1)
+        load_x(2)
         for quadrant in range(4):
             nc.sync.dma_start(
                 out=w2_planes[32 * quadrant : 32 * quadrant + 16, :].bitcast(I32),
                 in_=w2_scale_rows[4 * quadrant : 4 * quadrant + 4, :].rearrange("r (j c) -> j r c", j=PLANES),
             )
         load_w2_words(0)
-        load_x(2)
         load_w2_words(1)
         load_x(3)
 
@@ -150,36 +151,31 @@ def tile_multiheadlatentattention_pb_kernel(
             else:
                 nc.scalar.copy(out=out, in_=in_)
 
-        def transpose_x(i):
+        def transpose_x(i, half):
             pairs = x_sb[i][:].bitcast(F32)
-            x_t = []
-            for half in range(2):
-                x_t_half = wide_psum.tile([P, 2, 2, P], F32, tag="wide")
-                for g2 in range(2):
-                    g = 2 * half + g2
-                    for u in range(2):
-                        nc.tensor.transpose(
-                            x_t_half[:, g2, u, :], pairs[:, 256 * g + u : 256 * (g + 1) : 2], ident_f32[:]
-                        )
-                x_t.append(x_t_half)
-            return x_t
+            x_t_half = wide_psum.tile([P, 2, 2, P], F32, tag="wide")
+            for g2 in range(2):
+                g = 2 * half + g2
+                for u in range(2):
+                    nc.tensor.transpose(
+                        x_t_half[:, g2, u, :], pairs[:, 256 * g + u : 256 * (g + 1) : 2], ident_f32[:]
+                    )
+            return x_t_half
 
-        def group_x(i, x_t):
-            for half in range(2):
-                copy_out_of_psum(
-                    half == 0,
-                    out=x_grouped[i][:, 2 * half : 2 * half + 2, :, :].bitcast(F32),
-                    in_=x_t[half][:].rearrange("p g u k -> p g k u"),
-                )
+        def group_x(i, half, x_t_half, on_vector):
+            copy_out_of_psum(
+                on_vector,
+                out=x_grouped[i][:, 2 * half : 2 * half + 2, :, :].bitcast(F32),
+                in_=x_t_half[:].rearrange("p g u k -> p g k u"),
+            )
 
-        def quantise_x(i):
-            for half in range(2):
-                cols = slice(2 * P * half, 2 * P * (half + 1))
-                nc.vector.quantize_mx(
-                    out=x_codes[i][:, cols].bitcast(FP8X4),
-                    scales=x_scales[i][:, cols],
-                    in_=x_grouped[i][:, 2 * half : 2 * half + 2, :, :].rearrange("p g k t -> p (g k t)"),
-                )
+        def quantise_x(i, half):
+            cols = slice(2 * P * half, 2 * P * (half + 1))
+            nc.vector.quantize_mx(
+                out=x_codes[i][:, cols].bitcast(FP8X4),
+                scales=x_scales[i][:, cols],
+                in_=x_grouped[i][:, 2 * half : 2 * half + 2, :, :].rearrange("p g k t -> p (g k t)"),
+            )
 
         def first_matmul(i):
             latent = latent_psum.tile([P, LATENT], F32)
@@ -198,7 +194,7 @@ def tile_multiheadlatentattention_pb_kernel(
                     )
             return latent, raw_rope
 
-        def rotate(raw_rope):
+        def rotate_products(raw_rope):
             by_parity = raw_rope[:].rearrange("p (j e) -> p e j", e=2)
             from_even = work.tile([P, 2, HALF], F32)
             nc.vector.tensor_tensor(
@@ -208,6 +204,9 @@ def tile_multiheadlatentattention_pb_kernel(
             nc.vector.tensor_tensor(
                 out=from_odd[:], in0=by_parity[:, 1:2, :].to_broadcast([P, 2, HALF]), in1=table[:, 2:4, :], op=ALU.mult
             )
+            return from_even, from_odd
+
+        def rotate_sum(from_even, from_odd):
             rotated = work.tile([P, HALF, 2], F32)
             nc.vector.tensor_tensor(
                 out=rotated[:],
@@ -250,10 +249,13 @@ def tile_multiheadlatentattention_pb_kernel(
             )
             return c_sb
 
-        def quantise_c(i, c_sb):
+        def transpose_c(c_sb):
             c_t = narrow_psum.tile([P, PACK, P], BF16, tag="narrow")
             for t in range(PACK):
                 nc.tensor.transpose(c_t[:, t, :], c_sb[:, t, :], ident_bf16[:])
+            return c_t
+
+        def quantise_c(i, c_t):
             c_grouped = work.tile([P, P, PACK], BF16, align_bytes=64)
             nc.vector.tensor_copy(out=c_grouped[:], in_=c_t[:].rearrange("p t k -> p k t"))
             nc.vector.quantize_mx(
@@ -262,8 +264,8 @@ def tile_multiheadlatentattention_pb_kernel(
                 in_=c_grouped[:].rearrange("p k t -> p (k t)"),
             )
 
-        def second_matmul(i, half):
-            for bank in range(KV_BANKS // 2 * half, KV_BANKS // 2 * (half + 1)):
+        def second_matmul(i, first_bank, banks):
+            for bank in range(first_bank, first_bank + banks):
                 kv = wide_psum.tile([P, HEADS_PER_BANK, 2, HEAD_DIM], F32, tag="wide")
                 plane = (BANK * bank) // PLANE_COLS
                 plane_cols = slice((BANK * bank) % PLANE_COLS, (BANK * bank) % PLANE_COLS + BANK)
@@ -277,7 +279,7 @@ def tile_multiheadlatentattention_pb_kernel(
                     stop=True,
                 )
                 heads = slice(HEADS_PER_BANK * bank, HEADS_PER_BANK * (bank + 1))
-                on_vector = bank % 3 == 0
+                on_vector = bank in VECTOR_BANKS
                 copy_out_of_psum(on_vector, out=k_sb[i][:, heads, 0:HEAD_DIM], in_=kv[:, :, 0, :])
                 copy_out_of_psum(on_vector, out=v_sb[i][:, heads, :], in_=kv[:, :, 1, :])
 
@@ -292,32 +294,53 @@ def tile_multiheadlatentattention_pb_kernel(
                 in_=v_sb[i][:, stored, :].rearrange("p h d -> p (h d)"),
             )
 
-        group_x(0, transpose_x(0))
-        quantise_x(0)
+        for half in range(2):
+            group_x(0, half, transpose_x(0, half), half == 0)
+        for half in range(2):
+            quantise_x(0, half)
+        for half in range(2):
+            group_x(1, half, transpose_x(1, half), False)
         spread_gain()
+        for half in range(2):
+            quantise_x(1, half)
         latent, raw_rope = first_matmul(0)
-        rotated = rotate(raw_rope)
         inv_rms = inverse_rms(latent)
-        group_x(1, transpose_x(1))
+        group_x(2, 0, transpose_x(2, 0), False)
+        from_even, from_odd = rotate_products(raw_rope)
         c_sb = scale_c(latent, inv_rms)
+        rotated = rotate_sum(from_even, from_odd)
         repeat_rotated(0, rotated)
-        quantise_x(1)
+
         for i in range(TILES):
-            quantise_c(i, c_sb)
+            c_t = transpose_c(c_sb)
+            quantise_c(i, c_t)
             if i + 1 < TILES:
                 latent, raw_rope = first_matmul(i + 1)
-                rotated = rotate(raw_rope)
+                from_even, from_odd = rotate_products(raw_rope)
+                rotated = rotate_sum(from_even, from_odd)
                 inv_rms = inverse_rms(latent)
-            second_matmul(i, 0)
-            if i < TILES_STORED_BY_HALVES:
-                store(i, 0, HALF_HEADS)
+            if i == 0:
+                second_matmul(i, 0, 2)
+                store(i, 0, 4)
+                second_matmul(i, 2, 2)
+                store(i, 4, 4)
+            else:
+                second_matmul(i, 0, 4)
+                if i < TILES_STORED_BY_HALVES:
+                    store(i, 0, HALF_HEADS)
             if i + 1 < TILES:
                 c_sb = scale_c(latent, inv_rms)
                 repeat_rotated(i + 1, rotated)
-            if i + 2 < TILES:
-                group_x(i + 2, transpose_x(i + 2))
-                quantise_x(i + 2)
-            second_matmul(i, 1)
+            if i == 0:
+                group_x(2, 1, transpose_x(2, 1), False)
+                quantise_x(2, 0)
+                quantise_x(2, 1)
+            if i == 1:
+                for half in range(2):
+                    group_x(3, half, transpose_x(3, half), half == 0)
+                for half in range(2):
+                    quantise_x(3, half)
+            second_matmul(i, 4, 4)
             if i < TILES_STORED_BY_HALVES:
                 store(i, HALF_HEADS, HALF_HEADS)
             else:

@@ -305,7 +305,8 @@ def tile_multiheadlatentattention_pb_kernel(
             quantise_x(1, half)
         latent, raw_rope = first_matmul(0)
         inv_rms = inverse_rms(latent)
-        group_x(2, 0, transpose_x(2, 0), False)
+        for half in range(2):
+            group_x(2, half, transpose_x(2, half), False)
         from_even, from_odd = rotate_products(raw_rope)
         c_sb = scale_c(latent, inv_rms)
         rotated = rotate_sum(from_even, from_odd)
@@ -332,7 +333,6 @@ def tile_multiheadlatentattention_pb_kernel(
                 c_sb = scale_c(latent, inv_rms)
                 repeat_rotated(i + 1, rotated)
             if i == 0:
-                group_x(2, 1, transpose_x(2, 1), False)
                 quantise_x(2, 0)
                 quantise_x(2, 1)
             if i == 1:

@@ -69,6 +69,9 @@ def tile_multiheadlatentattention_pb_kernel(
         k_sb = [keep.tile([P, HEADS, 2 * HEAD_DIM], F32, name="k_sb%d" % i) for i in range(TILES)]
         v_sb = [keep.tile([P, HEADS, HEAD_DIM], F32, name="v_sb%d" % i) for i in range(TILES)]
 
+        idle = keep.tile([P, BANK], BF16)
+        nc.vector.memset(idle[:].bitcast(I32), 0)
+
         nc.vector.memset(w1_planes[:].bitcast(I32), 0)
         nc.vector.memset(w2_planes[:].bitcast(I32), 0)
 
@@ -145,6 +148,10 @@ def tile_multiheadlatentattention_pb_kernel(
             nc.tensor.matmul(out=gain_psum[:], lhsT=ones[:], rhs=gain_row[:], start=True, stop=True)
             nc.vector.tensor_copy(out=gain[:], in_=gain_psum[:].rearrange("p (q t) -> p t q", t=PACK))
 
+        def keep_clock(psum_tile, passes):
+            for step in range(passes):
+                nc.tensor.matmul(out=psum_tile[:], lhsT=idle[:, 0:P], rhs=idle[:], start=True, stop=True)
+
         def copy_out_of_psum(on_vector, out, in_):
             if on_vector:
                 nc.vector.tensor_copy(out=out, in_=in_)
@@ -178,7 +185,7 @@ def tile_multiheadlatentattention_pb_kernel(
             )
 
         def first_matmul(i):
-            latent = latent_psum.tile([P, LATENT], F32)
+            latent = latent_psum.tile([P, LATENT], F32, tag="latent")
             raw_rope = narrow_psum.tile([P, ROPE], F32, tag="narrow")
             for acc, cols in ((latent, slice(0, LATENT)), (raw_rope, slice(LATENT, A_COLS))):
                 for g in range(X_PASSES):
@@ -294,19 +301,25 @@ def tile_multiheadlatentattention_pb_kernel(
                 in_=v_sb[i][:, stored, :].rearrange("p h d -> p (h d)"),
             )
 
+        clock_bank = latent_psum.tile([P, LATENT], F32, tag="latent")
+        keep_clock(clock_bank, 6)
         for half in range(2):
             group_x(0, half, transpose_x(0, half), half == 0)
         for half in range(2):
             quantise_x(0, half)
+        keep_clock(clock_bank, 2)
         for half in range(2):
             group_x(1, half, transpose_x(1, half), False)
         spread_gain()
+        keep_clock(clock_bank, 1)
         for half in range(2):
             quantise_x(1, half)
         latent, raw_rope = first_matmul(0)
         inv_rms = inverse_rms(latent)
         for half in range(2):
             group_x(2, half, transpose_x(2, half), False)
+        clock_bank = wide_psum.tile([P, BANK], F32, tag="wide")
+        keep_clock(clock_bank, 2)
         from_even, from_odd = rotate_products(raw_rope)
         c_sb = scale_c(latent, inv_rms)
         rotated = rotate_sum(from_even, from_odd)

@@ -32,8 +32,7 @@ HEADS_PER_BANK = BANK // (2 * HEAD_DIM)
 PLANES = 4
 PLANE_COLS = KV_COLS // PLANES
 HALF_HEADS = HEADS // 2
-VECTOR_BANKS = (0, 3, 6)
-TILES_STORED_BY_HALVES = 2
+VECTOR_BANKS = (1, 3, 7)
 THETA = 10000.0
 EPS = 1e-6
 ROUND_MAGIC = 1.5 * 2.0**23
@@ -88,7 +87,6 @@ def tile_multiheadlatentattention_pb_kernel(
             nc.sync.dma_start(out=w2_words[:, cols].bitcast(I32), in_=w2_word_rows[:, cols])
 
         load_x(0)
-        load_x(1)
         for quadrant in range(4):
             nc.sync.dma_start(
                 out=w1_planes[32 * quadrant : 32 * quadrant + 16, :].bitcast(I32),
@@ -98,13 +96,14 @@ def tile_multiheadlatentattention_pb_kernel(
             nc.sync.dma_start(
                 out=w1_words[:, g : g + 2, :].bitcast(I32), in_=w1_word_rows[g : g + 2].rearrange("g p w -> p g w")
             )
-        load_x(2)
+        load_x(1)
         for quadrant in range(4):
             nc.sync.dma_start(
                 out=w2_planes[32 * quadrant : 32 * quadrant + 16, :].bitcast(I32),
                 in_=w2_scale_rows[4 * quadrant : 4 * quadrant + 4, :].rearrange("r (j c) -> j r c", j=PLANES),
             )
         load_w2_words(0)
+        load_x(2)
         load_w2_words(1)
         load_x(3)
 
@@ -120,6 +119,8 @@ def tile_multiheadlatentattention_pb_kernel(
         ident_bf16 = keep.tile([P, P], BF16)
         masks.make_identity(nc, ident_bf16[:])
 
+        sin_warm = keep.tile([P, 1], F32)
+        nc.scalar.activation(out=sin_warm[:], in_=idle[:, 0:1], func=ACT.Sin)
         turns = keep.tile([P, 2, HALF], F32)
         nc.vector.tensor_scalar_mul(out=turns[:, 1, 0:1], in0=position[:], scalar1=1.0 / (2.0 * math.pi))
         for doubling in range(6):
@@ -302,37 +303,31 @@ def tile_multiheadlatentattention_pb_kernel(
             )
 
         clock_bank = latent_psum.tile([P, LATENT], F32, tag="latent")
-        keep_clock(clock_bank, 6)
+        keep_clock(clock_bank, 5)
         for half in range(2):
             group_x(0, half, transpose_x(0, half), half == 0)
         for half in range(2):
             quantise_x(0, half)
-        keep_clock(clock_bank, 2)
-        for half in range(2):
-            group_x(1, half, transpose_x(1, half), False)
         spread_gain()
         keep_clock(clock_bank, 1)
-        for half in range(2):
-            quantise_x(1, half)
         latent, raw_rope = first_matmul(0)
         inv_rms = inverse_rms(latent)
         for half in range(2):
-            group_x(2, half, transpose_x(2, half), False)
+            group_x(1, half, transpose_x(1, half), False)
         clock_bank = wide_psum.tile([P, BANK], F32, tag="wide")
-        keep_clock(clock_bank, 2)
+        keep_clock(clock_bank, 1)
         from_even, from_odd = rotate_products(raw_rope)
         c_sb = scale_c(latent, inv_rms)
         rotated = rotate_sum(from_even, from_odd)
         repeat_rotated(0, rotated)
+        c_t = transpose_c(c_sb)
+        quantise_c(0, c_t)
+        for half in range(2):
+            quantise_x(1, half)
+        clock_bank = wide_psum.tile([P, BANK], F32, tag="wide")
+        keep_clock(clock_bank, 2)
 
         for i in range(TILES):
-            c_t = transpose_c(c_sb)
-            quantise_c(i, c_t)
-            if i + 1 < TILES:
-                latent, raw_rope = first_matmul(i + 1)
-                from_even, from_odd = rotate_products(raw_rope)
-                rotated = rotate_sum(from_even, from_odd)
-                inv_rms = inverse_rms(latent)
             if i == 0:
                 second_matmul(i, 0, 2)
                 store(i, 0, 4)
@@ -340,21 +335,28 @@ def tile_multiheadlatentattention_pb_kernel(
                 store(i, 4, 4)
             else:
                 second_matmul(i, 0, 4)
-                if i < TILES_STORED_BY_HALVES:
-                    store(i, 0, HALF_HEADS)
+                store(i, 0, HALF_HEADS)
             if i + 1 < TILES:
+                latent, raw_rope = first_matmul(i + 1)
+                inv_rms = inverse_rms(latent)
+                from_even, from_odd = rotate_products(raw_rope)
                 c_sb = scale_c(latent, inv_rms)
+                rotated = rotate_sum(from_even, from_odd)
                 repeat_rotated(i + 1, rotated)
-            if i == 0:
-                quantise_x(2, 0)
-                quantise_x(2, 1)
-            if i == 1:
-                for half in range(2):
-                    group_x(3, half, transpose_x(3, half), half == 0)
-                for half in range(2):
-                    quantise_x(3, half)
             second_matmul(i, 4, 4)
-            if i < TILES_STORED_BY_HALVES:
-                store(i, HALF_HEADS, HALF_HEADS)
-            else:
-                store(i, 0, HEADS)
+            store(i, HALF_HEADS, HALF_HEADS)
+            x_t_halves = []
+            if i + 2 < TILES:
+                x_t_halves.append(transpose_x(i + 2, 0))
+            if i + 1 < TILES:
+                c_t = transpose_c(c_sb)
+            if i + 2 < TILES:
+                x_t_halves.append(transpose_x(i + 2, 1))
+            if i + 1 < TILES:
+                clock_bank = latent_psum.tile([P, LATENT], F32, tag="latent")
+                keep_clock(clock_bank, 2)
+                quantise_c(i + 1, c_t)
+            for half, x_t_half in enumerate(x_t_halves):
+                group_x(i + 2, half, x_t_half, False)
+            for half in range(len(x_t_halves)):
+                quantise_x(i + 2, half)

@@ -53,7 +53,8 @@ def tile_multiheadlatentattention_pb_kernel(
         ctx.enter_context(tc.manual_schedule())
 
         x_sb = [keep.tile([P, C], BF16, name="x_sb%d" % i) for i in range(TILES)]
-        w1_words = keep.tile([P, X_PASSES, A_COLS], U32, align_bytes=64)
+        w1_words = keep.tile([P, X_PASSES, LATENT], U32, align_bytes=64)
+        w1_rope_words = keep.tile([P, X_PASSES, ROPE], U32, align_bytes=64)
         w2_words = keep.tile([P, KV_COLS], U32, align_bytes=64)
         w1_planes = keep.tile([P, A_COLS], U8, align_bytes=64)
         w2_planes = keep.tile([P, PLANE_COLS], U8, align_bytes=64)
@@ -68,11 +69,49 @@ def tile_multiheadlatentattention_pb_kernel(
         k_sb = [keep.tile([P, HEADS, 2 * HEAD_DIM], F32, name="k_sb%d" % i) for i in range(TILES)]
         v_sb = [keep.tile([P, HEADS, HEAD_DIM], F32, name="v_sb%d" % i) for i in range(TILES)]
 
-        idle = keep.tile([P, BANK], BF16)
-        nc.vector.memset(idle[:].bitcast(I32), 0)
-
         nc.vector.memset(w1_planes[:].bitcast(I32), 0)
+        gain_row = keep.tile([P, LATENT], BF16)
+        nc.vector.memset(gain_row[:].bitcast(I32), 0)
+        position = keep.tile([P, 1], I32)
+        nc.gpsimd.iota(position[:], pattern=[[0, 1]], base=0, channel_multiplier=1)
+        warm_in = keep.tile([P, 1], F32)
+        nc.gpsimd.memset(warm_in[:], 0.0)
+        warm = keep.tile([P, 1], F32)
+        nc.scalar.activation(out=warm[:], in_=warm_in[:], func=ACT.Sin)
+        idle = keep.tile([P, BANK], BF16)
+        nc.gpsimd.memset(idle[:], 0.0)
+        ident_f32 = keep.tile([P, P], F32)
+        masks.make_identity(nc, ident_f32[:])
+        ones = keep.tile([P, P], BF16)
+        nc.gpsimd.memset(ones[:], 1.0)
+        ident_bf16 = keep.tile([P, P], BF16)
+        masks.make_identity(nc, ident_bf16[:])
+
+        turns = keep.tile([P, 2, HALF], F32)
+        for j in range(4):
+            nc.vector.tensor_scalar_mul(
+                out=turns[:, 1, j : j + 1], in0=position[:], scalar1=THETA ** (-j / HALF) / (2.0 * math.pi)
+            )
+        for width in (4, 16):
+            for step in range(1, 4):
+                nc.vector.tensor_scalar_mul(
+                    out=turns[:, 1, width * step : width * (step + 1)],
+                    in0=turns[:, 1, 0:width],
+                    scalar1=THETA ** (-width * step / HALF),
+                )
+        nc.vector.tensor_scalar_add(out=turns[:, 0, :], in0=turns[:, 1, :], scalar1=0.25)
+        whole_turns = keep.tile([P, 2, HALF], F32)
+        nc.vector.tensor_scalar(
+            out=whole_turns[:], in0=turns[:], scalar1=ROUND_MAGIC, scalar2=ROUND_MAGIC, op0=ALU.add, op1=ALU.subtract
+        )
+        part_turns = keep.tile([P, 2, HALF], F32)
+        nc.vector.tensor_sub(out=part_turns[:], in0=turns[:], in1=whole_turns[:])
         nc.vector.memset(w2_planes[:].bitcast(I32), 0)
+        table = keep.tile([P, 4, HALF], F32)
+        nc.scalar.activation(out=table[:, 0:2, :], in_=part_turns[:], func=ACT.Sin, scale=2.0 * math.pi)
+        nc.vector.tensor_scalar_mul(out=table[:, 2, :], in0=table[:, 1, :], scalar1=-1.0)
+        nc.vector.tensor_copy(out=table[:, 3, :], in_=table[:, 0, :])
+        nc.scalar.activation(out=warm[:], in_=table[:, 0, 0:1], func=ACT.Abs_reciprocal_sqrt, scale=0.0, bias=1.0)
 
         w1_scale_rows = w_kva_scales.bitcast(I32)
         w2_scale_rows = w_kvb_scales[0].bitcast(I32)
@@ -87,6 +126,7 @@ def tile_multiheadlatentattention_pb_kernel(
             nc.sync.dma_start(out=w2_words[:, cols].bitcast(I32), in_=w2_word_rows[:, cols])
 
         load_x(0)
+        nc.sync.dma_start(out=gain_row[0:1, :], in_=kva_norm_w.unsqueeze(0))
         for quadrant in range(4):
             nc.sync.dma_start(
                 out=w1_planes[32 * quadrant : 32 * quadrant + 16, :].bitcast(I32),
@@ -94,9 +134,13 @@ def tile_multiheadlatentattention_pb_kernel(
             )
         for g in range(0, X_PASSES, 2):
             nc.sync.dma_start(
-                out=w1_words[:, g : g + 2, :].bitcast(I32), in_=w1_word_rows[g : g + 2].rearrange("g p w -> p g w")
+                out=w1_words[:, g : g + 2, :].bitcast(I32),
+                in_=w1_word_rows[g : g + 2, :, 0:LATENT].rearrange("g p w -> p g w"),
             )
         load_x(1)
+        nc.sync.dma_start(
+            out=w1_rope_words[:].bitcast(I32), in_=w1_word_rows[:, :, LATENT:].rearrange("g p w -> p g w")
+        )
         for quadrant in range(4):
             nc.sync.dma_start(
                 out=w2_planes[32 * quadrant : 32 * quadrant + 16, :].bitcast(I32),
@@ -106,41 +150,6 @@ def tile_multiheadlatentattention_pb_kernel(
         load_x(2)
         load_w2_words(1)
         load_x(3)
-
-        gain_row = keep.tile([P, LATENT], BF16)
-        nc.vector.memset(gain_row[:].bitcast(I32), 0)
-        nc.scalar.dma_start(out=gain_row[0:1, :], in_=kva_norm_w.unsqueeze(0))
-        position = keep.tile([P, 1], I32)
-        nc.gpsimd.iota(position[:], pattern=[[0, 1]], base=0, channel_multiplier=1)
-        ident_f32 = keep.tile([P, P], F32)
-        masks.make_identity(nc, ident_f32[:])
-        ones = keep.tile([P, P], BF16)
-        nc.gpsimd.memset(ones[:], 1.0)
-        ident_bf16 = keep.tile([P, P], BF16)
-        masks.make_identity(nc, ident_bf16[:])
-
-        sin_warm = keep.tile([P, 1], F32)
-        nc.scalar.activation(out=sin_warm[:], in_=idle[:, 0:1], func=ACT.Sin)
-        turns = keep.tile([P, 2, HALF], F32)
-        nc.vector.tensor_scalar_mul(out=turns[:, 1, 0:1], in0=position[:], scalar1=1.0 / (2.0 * math.pi))
-        for doubling in range(6):
-            width = 2**doubling
-            nc.vector.tensor_scalar_mul(
-                out=turns[:, 1, width : 2 * width], in0=turns[:, 1, 0:width], scalar1=THETA ** (-width / HALF)
-            )
-        nc.vector.tensor_scalar_add(out=turns[:, 0, :], in0=turns[:, 1, :], scalar1=0.25)
-        whole_turns = keep.tile([P, 2, HALF], F32)
-        nc.vector.tensor_scalar(
-            out=whole_turns[:], in0=turns[:], scalar1=ROUND_MAGIC, scalar2=ROUND_MAGIC, op0=ALU.add, op1=ALU.subtract
-        )
-        part_turns = keep.tile([P, 2, HALF], F32)
-        nc.vector.tensor_sub(out=part_turns[:], in0=turns[:], in1=whole_turns[:])
-        table = keep.tile([P, 4, HALF], F32)
-        nc.scalar.activation(out=table[:, 0:2, :], in_=part_turns[:], func=ACT.Sin, scale=2.0 * math.pi)
-        nc.vector.tensor_scalar_mul(out=table[:, 2, :], in0=table[:, 1, :], scalar1=-1.0)
-        nc.vector.tensor_copy(out=table[:, 3, :], in_=table[:, 0, :])
-        warm = keep.tile([P, 1], F32)
-        nc.scalar.activation(out=warm[:], in_=table[:, 0, 0:1], func=ACT.Abs_reciprocal_sqrt, scale=0.0, bias=1.0)
 
         gain = keep.tile([P, PACK, P], F32)
 
@@ -185,22 +194,28 @@ def tile_multiheadlatentattention_pb_kernel(
                 in_=x_grouped[i][:, 2 * half : 2 * half + 2, :, :].rearrange("p g k t -> p (g k t)"),
             )
 
-        def first_matmul(i):
+        def first_passes(i, acc, words, cols):
+            for g in range(X_PASSES):
+                tokens = slice(P * g, P * (g + 1))
+                nc.tensor.matmul_mx(
+                    out=acc[:],
+                    lhsT=x_codes[i][:, tokens].bitcast(FP8X4),
+                    lhsT_scale=x_scales[i][:, tokens],
+                    rhs=words[:, g, :].bitcast(FP8X4),
+                    rhs_scale=w1_planes[4 * g : P, cols],
+                    start=(g == 0),
+                    stop=(g == X_PASSES - 1),
+                )
+
+        def latent_matmul(i):
             latent = latent_psum.tile([P, LATENT], F32, tag="latent")
+            first_passes(i, latent, w1_words, slice(0, LATENT))
+            return latent
+
+        def rope_matmul(i):
             raw_rope = narrow_psum.tile([P, ROPE], F32, tag="narrow")
-            for acc, cols in ((latent, slice(0, LATENT)), (raw_rope, slice(LATENT, A_COLS))):
-                for g in range(X_PASSES):
-                    tokens = slice(P * g, P * (g + 1))
-                    nc.tensor.matmul_mx(
-                        out=acc[:],
-                        lhsT=x_codes[i][:, tokens].bitcast(FP8X4),
-                        lhsT_scale=x_scales[i][:, tokens],
-                        rhs=w1_words[:, g, cols].bitcast(FP8X4),
-                        rhs_scale=w1_planes[4 * g : P, cols],
-                        start=(g == 0),
-                        stop=(g == X_PASSES - 1),
-                    )
-            return latent, raw_rope
+            first_passes(i, raw_rope, w1_rope_words, slice(LATENT, A_COLS))
+            return raw_rope
 
         def rotate_products(raw_rope):
             by_parity = raw_rope[:].rearrange("p (j e) -> p e j", e=2)
@@ -303,42 +318,46 @@ def tile_multiheadlatentattention_pb_kernel(
             )
 
         clock_bank = latent_psum.tile([P, LATENT], F32, tag="latent")
-        keep_clock(clock_bank, 5)
+        keep_clock(clock_bank, 4)
         for half in range(2):
             group_x(0, half, transpose_x(0, half), half == 0)
         for half in range(2):
             quantise_x(0, half)
-        spread_gain()
         keep_clock(clock_bank, 1)
-        latent, raw_rope = first_matmul(0)
+        spread_gain()
+        latent = latent_matmul(0)
         inv_rms = inverse_rms(latent)
         for half in range(2):
             group_x(1, half, transpose_x(1, half), False)
+        raw_rope = rope_matmul(0)
         clock_bank = wide_psum.tile([P, BANK], F32, tag="wide")
         keep_clock(clock_bank, 1)
-        from_even, from_odd = rotate_products(raw_rope)
         c_sb = scale_c(latent, inv_rms)
+        from_even, from_odd = rotate_products(raw_rope)
+        c_t = transpose_c(c_sb)
+        quantise_x(1, 0)
         rotated = rotate_sum(from_even, from_odd)
         repeat_rotated(0, rotated)
-        c_t = transpose_c(c_sb)
+        quantise_x(1, 1)
         quantise_c(0, c_t)
-        for half in range(2):
-            quantise_x(1, half)
-        clock_bank = wide_psum.tile([P, BANK], F32, tag="wide")
-        keep_clock(clock_bank, 2)
+        latent = latent_matmul(1)
 
         for i in range(TILES):
             if i == 0:
                 second_matmul(i, 0, 2)
                 store(i, 0, 4)
+                raw_rope = rope_matmul(1)
+                inv_rms = inverse_rms(latent)
                 second_matmul(i, 2, 2)
                 store(i, 4, 4)
             else:
                 second_matmul(i, 0, 4)
                 store(i, 0, HALF_HEADS)
+                if i + 1 < TILES:
+                    latent = latent_matmul(i + 1)
+                    raw_rope = rope_matmul(i + 1)
+                    inv_rms = inverse_rms(latent)
             if i + 1 < TILES:
-                latent, raw_rope = first_matmul(i + 1)
-                inv_rms = inverse_rms(latent)
                 from_even, from_odd = rotate_products(raw_rope)
                 c_sb = scale_c(latent, inv_rms)
                 rotated = rotate_sum(from_even, from_odd)
@@ -356,7 +375,7 @@ def tile_multiheadlatentattention_pb_kernel(
                 clock_bank = latent_psum.tile([P, LATENT], F32, tag="latent")
                 keep_clock(clock_bank, 2)
                 quantise_c(i + 1, c_t)
-            for half, x_t_half in enumerate(x_t_halves):
-                group_x(i + 2, half, x_t_half, False)
+            for half in range(len(x_t_halves)):
+                group_x(i + 2, half, x_t_halves[half], False)
             for half in range(len(x_t_halves)):
                 quantise_x(i + 2, half)

@@ -28,6 +28,7 @@ HEAD_DIM = 128
 KV_COLS = HEADS * 2 * HEAD_DIM
 BANK = 512
 KV_BANKS = KV_COLS // BANK
+HALVES = ([0, 1], [2, 3])
 HEADS_PER_BANK = BANK // (2 * HEAD_DIM)
 PLANES = 4
 PLANE_COLS = KV_COLS // PLANES
@@ -108,10 +109,12 @@ def tile_multiheadlatentattention_pb_kernel(
         nc.vector.tensor_sub(out=part_turns[:], in0=turns[:], in1=whole_turns[:])
         nc.vector.memset(w2_planes[:].bitcast(I32), 0)
         table = keep.tile([P, 4, HALF], F32)
-        nc.scalar.activation(out=table[:, 0:2, :], in_=part_turns[:], func=ACT.Sin, scale=2.0 * math.pi)
-        nc.vector.tensor_scalar_mul(out=table[:, 2, :], in0=table[:, 1, :], scalar1=-1.0)
-        nc.vector.tensor_copy(out=table[:, 3, :], in_=table[:, 0, :])
-        nc.scalar.activation(out=warm[:], in_=table[:, 0, 0:1], func=ACT.Abs_reciprocal_sqrt, scale=0.0, bias=1.0)
+
+        def finish_tables():
+            nc.scalar.activation(out=table[:, 0:2, :], in_=part_turns[:], func=ACT.Sin, scale=2.0 * math.pi)
+            nc.vector.tensor_scalar_mul(out=table[:, 2, :], in0=table[:, 1, :], scalar1=-1.0)
+            nc.vector.tensor_copy(out=table[:, 3, :], in_=table[:, 0, :])
+            nc.scalar.activation(out=warm[:], in_=table[:, 0, 0:1], func=ACT.Abs_reciprocal_sqrt, scale=0.0, bias=1.0)
 
         w1_scale_rows = w_kva_scales.bitcast(I32)
         w2_scale_rows = w_kvb_scales[0].bitcast(I32)
@@ -168,30 +171,27 @@ def tile_multiheadlatentattention_pb_kernel(
             else:
                 nc.scalar.copy(out=out, in_=in_)
 
-        def transpose_x(i, half):
+        def transpose_x(i, passes):
             pairs = x_sb[i][:].bitcast(F32)
-            x_t_half = wide_psum.tile([P, 2, 2, P], F32, tag="wide")
-            for g2 in range(2):
-                g = 2 * half + g2
+            x_t = wide_psum.tile([P, len(passes), 2, P], F32, tag="wide")
+            for index, g in enumerate(passes):
                 for u in range(2):
-                    nc.tensor.transpose(
-                        x_t_half[:, g2, u, :], pairs[:, 256 * g + u : 256 * (g + 1) : 2], ident_f32[:]
-                    )
-            return x_t_half
+                    nc.tensor.transpose(x_t[:, index, u, :], pairs[:, 256 * g + u : 256 * (g + 1) : 2], ident_f32[:])
+            return x_t
 
-        def group_x(i, half, x_t_half, on_vector):
+        def group_x(i, passes, x_t, on_vector):
             copy_out_of_psum(
                 on_vector,
-                out=x_grouped[i][:, 2 * half : 2 * half + 2, :, :].bitcast(F32),
-                in_=x_t_half[:].rearrange("p g u k -> p g k u"),
+                out=x_grouped[i][:, passes[0] : passes[-1] + 1, :, :].bitcast(F32),
+                in_=x_t[:].rearrange("p g u k -> p g k u"),
             )
 
-        def quantise_x(i, half):
-            cols = slice(2 * P * half, 2 * P * (half + 1))
+        def quantise_x(i, passes):
+            cols = slice(P * passes[0], P * (passes[-1] + 1))
             nc.vector.quantize_mx(
                 out=x_codes[i][:, cols].bitcast(FP8X4),
                 scales=x_scales[i][:, cols],
-                in_=x_grouped[i][:, 2 * half : 2 * half + 2, :, :].rearrange("p g k t -> p (g k t)"),
+                in_=x_grouped[i][:, passes[0] : passes[-1] + 1, :, :].rearrange("p g k t -> p (g k t)"),
             )
 
         def first_passes(i, acc, words, cols):
@@ -319,27 +319,27 @@ def tile_multiheadlatentattention_pb_kernel(
 
         clock_bank = latent_psum.tile([P, LATENT], F32, tag="latent")
         keep_clock(clock_bank, 4)
-        for half in range(2):
-            group_x(0, half, transpose_x(0, half), half == 0)
-        for half in range(2):
-            quantise_x(0, half)
+        for g in range(X_PASSES):
+            group_x(0, [g], transpose_x(0, [g]), g % 2 == 0)
+            quantise_x(0, [g])
+        finish_tables()
         keep_clock(clock_bank, 1)
         spread_gain()
         latent = latent_matmul(0)
         inv_rms = inverse_rms(latent)
-        for half in range(2):
-            group_x(1, half, transpose_x(1, half), False)
+        for passes in HALVES:
+            group_x(1, passes, transpose_x(1, passes), False)
         raw_rope = rope_matmul(0)
         clock_bank = wide_psum.tile([P, BANK], F32, tag="wide")
         keep_clock(clock_bank, 1)
         c_sb = scale_c(latent, inv_rms)
         from_even, from_odd = rotate_products(raw_rope)
         c_t = transpose_c(c_sb)
-        quantise_x(1, 0)
+        for passes in HALVES:
+            quantise_x(1, passes)
+        quantise_c(0, c_t)
         rotated = rotate_sum(from_even, from_odd)
         repeat_rotated(0, rotated)
-        quantise_x(1, 1)
-        quantise_c(0, c_t)
         latent = latent_matmul(1)
 
         for i in range(TILES):
@@ -360,22 +360,23 @@ def tile_multiheadlatentattention_pb_kernel(
             if i + 1 < TILES:
                 from_even, from_odd = rotate_products(raw_rope)
                 c_sb = scale_c(latent, inv_rms)
-                rotated = rotate_sum(from_even, from_odd)
-                repeat_rotated(i + 1, rotated)
             second_matmul(i, 4, 4)
             store(i, HALF_HEADS, HALF_HEADS)
-            x_t_halves = []
+            x_ts = []
             if i + 2 < TILES:
-                x_t_halves.append(transpose_x(i + 2, 0))
+                x_ts.append(transpose_x(i + 2, HALVES[0]))
             if i + 1 < TILES:
                 c_t = transpose_c(c_sb)
             if i + 2 < TILES:
-                x_t_halves.append(transpose_x(i + 2, 1))
+                x_ts.append(transpose_x(i + 2, HALVES[1]))
             if i + 1 < TILES:
                 clock_bank = latent_psum.tile([P, LATENT], F32, tag="latent")
                 keep_clock(clock_bank, 2)
                 quantise_c(i + 1, c_t)
-            for half in range(len(x_t_halves)):
-                group_x(i + 2, half, x_t_halves[half], False)
-            for half in range(len(x_t_halves)):
-                quantise_x(i + 2, half)
+                rotated = rotate_sum(from_even, from_odd)
+                repeat_rotated(i + 1, rotated)
+            for passes, x_t in zip(HALVES, x_ts):
+                group_x(i + 2, passes, x_t, False)
+            if i + 2 < TILES:
+                for passes in HALVES:
+                    quantise_x(i + 2, passes)

@@ -32,8 +32,9 @@ HALVES = ([0, 1], [2, 3])
 HEADS_PER_BANK = BANK // (2 * HEAD_DIM)
 PLANES = 4
 PLANE_COLS = KV_COLS // PLANES
+TILES_STORED_BY_HALVES = 2
 HALF_HEADS = HEADS // 2
-VECTOR_BANKS = (1, 3, 7)
+VECTOR_BANKS = (1, 3, 5)
 THETA = 10000.0
 EPS = 1e-6
 ROUND_MAGIC = 1.5 * 2.0**23
@@ -144,13 +145,13 @@ def tile_multiheadlatentattention_pb_kernel(
         nc.sync.dma_start(
             out=w1_rope_words[:].bitcast(I32), in_=w1_word_rows[:, :, LATENT:].rearrange("g p w -> p g w")
         )
+        load_x(2)
         for quadrant in range(4):
             nc.sync.dma_start(
                 out=w2_planes[32 * quadrant : 32 * quadrant + 16, :].bitcast(I32),
                 in_=w2_scale_rows[4 * quadrant : 4 * quadrant + 4, :].rearrange("r (j c) -> j r c", j=PLANES),
             )
         load_w2_words(0)
-        load_x(2)
         load_w2_words(1)
         load_x(3)
 
@@ -331,18 +332,26 @@ def tile_multiheadlatentattention_pb_kernel(
             group_x(1, passes, transpose_x(1, passes), False)
         raw_rope = rope_matmul(0)
         clock_bank = wide_psum.tile([P, BANK], F32, tag="wide")
-        keep_clock(clock_bank, 1)
+        keep_clock(clock_bank, 2)
         c_sb = scale_c(latent, inv_rms)
         from_even, from_odd = rotate_products(raw_rope)
-        c_t = transpose_c(c_sb)
-        for passes in HALVES:
-            quantise_x(1, passes)
-        quantise_c(0, c_t)
-        rotated = rotate_sum(from_even, from_odd)
-        repeat_rotated(0, rotated)
-        latent = latent_matmul(1)
 
         for i in range(TILES):
+            x_ts = []
+            if i == 0:
+                x_ts.append(transpose_x(2, HALVES[0]))
+            c_t = transpose_c(c_sb)
+            if i == 0:
+                x_ts.append(transpose_x(2, HALVES[1]))
+                for passes in HALVES:
+                    quantise_x(1, passes)
+            quantise_c(i, c_t)
+            rotated = rotate_sum(from_even, from_odd)
+            repeat_rotated(i, rotated)
+            for passes, x_t in zip(HALVES, x_ts):
+                group_x(2, passes, x_t, False)
+            if i + 1 < TILES:
+                latent = latent_matmul(i + 1)
             if i == 0:
                 second_matmul(i, 0, 2)
                 store(i, 0, 4)
@@ -350,33 +359,27 @@ def tile_multiheadlatentattention_pb_kernel(
                 inv_rms = inverse_rms(latent)
                 second_matmul(i, 2, 2)
                 store(i, 4, 4)
+                from_even, from_odd = rotate_products(raw_rope)
             else:
-                second_matmul(i, 0, 4)
-                store(i, 0, HALF_HEADS)
                 if i + 1 < TILES:
-                    latent = latent_matmul(i + 1)
                     raw_rope = rope_matmul(i + 1)
                     inv_rms = inverse_rms(latent)
+                    from_even, from_odd = rotate_products(raw_rope)
+                second_matmul(i, 0, 4)
+                if i < TILES_STORED_BY_HALVES:
+                    store(i, 0, HALF_HEADS)
             if i + 1 < TILES:
-                from_even, from_odd = rotate_products(raw_rope)
                 c_sb = scale_c(latent, inv_rms)
-            second_matmul(i, 4, 4)
-            store(i, HALF_HEADS, HALF_HEADS)
-            x_ts = []
-            if i + 2 < TILES:
-                x_ts.append(transpose_x(i + 2, HALVES[0]))
-            if i + 1 < TILES:
-                c_t = transpose_c(c_sb)
-            if i + 2 < TILES:
-                x_ts.append(transpose_x(i + 2, HALVES[1]))
-            if i + 1 < TILES:
-                clock_bank = latent_psum.tile([P, LATENT], F32, tag="latent")
-                keep_clock(clock_bank, 2)
-                quantise_c(i + 1, c_t)
-                rotated = rotate_sum(from_even, from_odd)
-                repeat_rotated(i + 1, rotated)
-            for passes, x_t in zip(HALVES, x_ts):
-                group_x(i + 2, passes, x_t, False)
-            if i + 2 < TILES:
+            if i == 0:
                 for passes in HALVES:
-                    quantise_x(i + 2, passes)
+                    quantise_x(2, passes)
+            if i == 1:
+                for passes in HALVES:
+                    group_x(3, passes, transpose_x(3, passes), passes == HALVES[0])
+                for passes in HALVES:
+                    quantise_x(3, passes)
+            second_matmul(i, 4, 4)
+            if i < TILES_STORED_BY_HALVES:
+                store(i, HALF_HEADS, HALF_HEADS)
+            else:
+                store(i, 0, HEADS)

@@ -122,6 +122,14 @@ def tile_multiheadlatentattention_pb_kernel(
         w1_word_rows = w_kva_words.rearrange("g p n t -> g p (n t)").bitcast(I32)
         w2_word_rows = w_kvb_words[0].rearrange("p n t -> p (n t)").bitcast(I32)
 
+        def load_w1_planes(cols):
+            words = slice(cols.start // 4, cols.stop // 4)
+            for quadrant in range(4):
+                nc.sync.dma_start(
+                    out=w1_planes[32 * quadrant : 32 * quadrant + 16, cols].bitcast(I32),
+                    in_=w1_scale_rows[:, 4 * quadrant : 4 * quadrant + 4, words],
+                )
+
         def load_x(i):
             nc.sync.dma_start(out=x_sb[i][:], in_=x[i])
 
@@ -131,17 +139,14 @@ def tile_multiheadlatentattention_pb_kernel(
 
         load_x(0)
         nc.sync.dma_start(out=gain_row[0:1, :], in_=kva_norm_w.unsqueeze(0))
-        for quadrant in range(4):
-            nc.sync.dma_start(
-                out=w1_planes[32 * quadrant : 32 * quadrant + 16, :].bitcast(I32),
-                in_=w1_scale_rows[:, 4 * quadrant : 4 * quadrant + 4, :],
-            )
+        load_w1_planes(slice(0, LATENT))
         for g in range(0, X_PASSES, 2):
             nc.sync.dma_start(
                 out=w1_words[:, g : g + 2, :].bitcast(I32),
                 in_=w1_word_rows[g : g + 2, :, 0:LATENT].rearrange("g p w -> p g w"),
             )
         load_x(1)
+        load_w1_planes(slice(LATENT, A_COLS))
         nc.sync.dma_start(
             out=w1_rope_words[:].bitcast(I32), in_=w1_word_rows[:, :, LATENT:].rearrange("g p w -> p g w")
         )
@@ -319,14 +324,17 @@ def tile_multiheadlatentattention_pb_kernel(
             )
 
         clock_bank = latent_psum.tile([P, LATENT], F32, tag="latent")
-        keep_clock(clock_bank, 4)
+        keep_clock(clock_bank, 6)
         for g in range(X_PASSES):
             group_x(0, [g], transpose_x(0, [g]), g % 2 == 0)
             quantise_x(0, [g])
+            if g % 2 == 1:
+                keep_clock(clock_bank, 1)
         finish_tables()
-        keep_clock(clock_bank, 1)
         spread_gain()
         latent = latent_matmul(0)
+        clock_bank = wide_psum.tile([P, BANK], F32, tag="wide")
+        keep_clock(clock_bank, 1)
         inv_rms = inverse_rms(latent)
         for passes in HALVES:
             group_x(1, passes, transpose_x(1, passes), False)

@@ -122,14 +122,6 @@ def tile_multiheadlatentattention_pb_kernel(
         w1_word_rows = w_kva_words.rearrange("g p n t -> g p (n t)").bitcast(I32)
         w2_word_rows = w_kvb_words[0].rearrange("p n t -> p (n t)").bitcast(I32)
 
-        def load_w1_planes(cols):
-            words = slice(cols.start // 4, cols.stop // 4)
-            for quadrant in range(4):
-                nc.sync.dma_start(
-                    out=w1_planes[32 * quadrant : 32 * quadrant + 16, cols].bitcast(I32),
-                    in_=w1_scale_rows[:, 4 * quadrant : 4 * quadrant + 4, words],
-                )
-
         def load_x(i):
             nc.sync.dma_start(out=x_sb[i][:], in_=x[i])
 
@@ -139,14 +131,17 @@ def tile_multiheadlatentattention_pb_kernel(
 
         load_x(0)
         nc.sync.dma_start(out=gain_row[0:1, :], in_=kva_norm_w.unsqueeze(0))
-        load_w1_planes(slice(0, LATENT))
+        for quadrant in range(4):
+            nc.sync.dma_start(
+                out=w1_planes[32 * quadrant : 32 * quadrant + 16, :].bitcast(I32),
+                in_=w1_scale_rows[:, 4 * quadrant : 4 * quadrant + 4, :],
+            )
         for g in range(0, X_PASSES, 2):
             nc.sync.dma_start(
                 out=w1_words[:, g : g + 2, :].bitcast(I32),
                 in_=w1_word_rows[g : g + 2, :, 0:LATENT].rearrange("g p w -> p g w"),
             )
         load_x(1)
-        load_w1_planes(slice(LATENT, A_COLS))
         nc.sync.dma_start(
             out=w1_rope_words[:].bitcast(I32), in_=w1_word_rows[:, :, LATENT:].rearrange("g p w -> p g w")
         )

import math
from contextlib import ExitStack

import concourse.masks as masks
import concourse.mybir as mybir

F32 = mybir.dt.float32
BF16 = mybir.dt.bfloat16
I32 = mybir.dt.int32
U32 = mybir.dt.uint32
U8 = mybir.dt.uint8
FP8X4 = mybir.dt.float8_e4m3fn_x4
ALU = mybir.AluOpType
ACT = mybir.ActivationFunctionType

P = 128
PACK = 4
K_PASS = P * PACK
TILES = 4
C = 2048
X_PASSES = C // K_PASS
LATENT = 512
ROPE = 128
HALF = ROPE // 2
A_COLS = LATENT + ROPE
HEADS = 16
HEAD_DIM = 128
KV_COLS = HEADS * 2 * HEAD_DIM
BANK = 512
KV_BANKS = KV_COLS // BANK
HALVES = ([0, 1], [2, 3])
HEADS_PER_BANK = BANK // (2 * HEAD_DIM)
PLANES = 4
PLANE_COLS = KV_COLS // PLANES
TILES_STORED_BY_HALVES = 2
HALF_HEADS = HEADS // 2
VECTOR_BANKS = (1, 3, 5)
THETA = 10000.0
EPS = 1e-6
ROUND_MAGIC = 1.5 * 2.0**23

FLOPS = 2 * TILES * P * (C * A_COLS + LATENT * KV_COLS)


def tile_multiheadlatentattention_pb_kernel(
    tc, x, w_kva_words, w_kva_scales, kva_norm_w, w_kvb_words, w_kvb_scales, out_0, out_1
):
    nc = tc.nc
    with ExitStack() as ctx:
        keep = ctx.enter_context(tc.tile_pool(name="keep", bufs=1))
        work = ctx.enter_context(tc.tile_pool(name="work", bufs=2))
        wide_psum = ctx.enter_context(tc.psum_pool(name="wide_psum", bufs=5))
        latent_psum = ctx.enter_context(tc.psum_pool(name="latent_psum", bufs=1))
        narrow_psum = ctx.enter_context(tc.psum_pool(name="narrow_psum", bufs=2))
        ctx.enter_context(tc.manual_schedule())

        x_sb = [keep.tile([P, C], BF16, name="x_sb%d" % i) for i in range(TILES)]
        w1_words = keep.tile([P, X_PASSES, LATENT], U32, align_bytes=64)
        w1_rope_words = keep.tile([P, X_PASSES, ROPE], U32, align_bytes=64)
        w2_words = keep.tile([P, KV_COLS], U32, align_bytes=64)
        w1_planes = keep.tile([P, A_COLS], U8, align_bytes=64)
        w2_planes = keep.tile([P, PLANE_COLS], U8, align_bytes=64)
        x_grouped = [
            keep.tile([P, X_PASSES, P, PACK], BF16, name="x_grouped%d" % i, align_bytes=64)
            for i in range(TILES)
        ]
        x_codes = [keep.tile([P, X_PASSES * P], U32, name="x_codes%d" % i, align_bytes=64) for i in range(TILES)]
        x_scales = [keep.tile([P, X_PASSES * P], U8, name="x_scales%d" % i, align_bytes=64) for i in range(TILES)]
        c_codes = [keep.tile([P, P], U32, name="c_codes%d" % i, align_bytes=64) for i in range(TILES)]
        c_scales = [keep.tile([P, P], U8, name="c_scales%d" % i, align_bytes=64) for i in range(TILES)]
        k_sb = [keep.tile([P, HEADS, 2 * HEAD_DIM], F32, name="k_sb%d" % i) for i in range(TILES)]
        v_sb = [keep.tile([P, HEADS, HEAD_DIM], F32, name="v_sb%d" % i) for i in range(TILES)]

        nc.vector.memset(w1_planes[:].bitcast(I32), 0)
        gain_row = keep.tile([P, LATENT], BF16)
        nc.vector.memset(gain_row[:].bitcast(I32), 0)
        position = keep.tile([P, 1], I32)
        nc.gpsimd.iota(position[:], pattern=[[0, 1]], base=0, channel_multiplier=1)
        warm_in = keep.tile([P, 1], F32)
        nc.gpsimd.memset(warm_in[:], 0.0)
        warm = keep.tile([P, 1], F32)
        nc.scalar.activation(out=warm[:], in_=warm_in[:], func=ACT.Sin)
        idle = keep.tile([P, BANK], BF16)
        nc.gpsimd.memset(idle[:], 0.0)
        ident_f32 = keep.tile([P, P], F32)
        masks.make_identity(nc, ident_f32[:])
        ones = keep.tile([P, P], BF16)
        nc.gpsimd.memset(ones[:], 1.0)
        ident_bf16 = keep.tile([P, P], BF16)
        masks.make_identity(nc, ident_bf16[:])

        turns = keep.tile([P, 2, HALF], F32)
        for j in range(4):
            nc.vector.tensor_scalar_mul(
                out=turns[:, 1, j : j + 1], in0=position[:], scalar1=THETA ** (-j / HALF) / (2.0 * math.pi)
            )
        for width in (4, 16):
            for step in range(1, 4):
                nc.vector.tensor_scalar_mul(
                    out=turns[:, 1, width * step : width * (step + 1)],
                    in0=turns[:, 1, 0:width],
                    scalar1=THETA ** (-width * step / HALF),
                )
        nc.vector.tensor_scalar_add(out=turns[:, 0, :], in0=turns[:, 1, :], scalar1=0.25)
        whole_turns = keep.tile([P, 2, HALF], F32)
        nc.vector.tensor_scalar(
            out=whole_turns[:], in0=turns[:], scalar1=ROUND_MAGIC, scalar2=ROUND_MAGIC, op0=ALU.add, op1=ALU.subtract
        )
        part_turns = keep.tile([P, 2, HALF], F32)
        nc.vector.tensor_sub(out=part_turns[:], in0=turns[:], in1=whole_turns[:])
        nc.vector.memset(w2_planes[:].bitcast(I32), 0)
        table = keep.tile([P, 4, HALF], F32)

        def finish_tables():
            nc.scalar.activation(out=table[:, 0:2, :], in_=part_turns[:], func=ACT.Sin, scale=2.0 * math.pi)
            nc.vector.tensor_scalar_mul(out=table[:, 2, :], in0=table[:, 1, :], scalar1=-1.0)
            nc.vector.tensor_copy(out=table[:, 3, :], in_=table[:, 0, :])
            nc.scalar.activation(out=warm[:], in_=table[:, 0, 0:1], func=ACT.Abs_reciprocal_sqrt, scale=0.0, bias=1.0)

        w1_scale_rows = w_kva_scales.bitcast(I32)
        w2_scale_rows = w_kvb_scales[0].bitcast(I32)
        w1_word_rows = w_kva_words.rearrange("g p n t -> g p (n t)").bitcast(I32)
        w2_word_rows = w_kvb_words[0].rearrange("p n t -> p (n t)").bitcast(I32)

        def load_x(i):
            nc.sync.dma_start(out=x_sb[i][:], in_=x[i])

        def load_w2_words(half):
            cols = slice(KV_COLS // 2 * half, KV_COLS // 2 * (half + 1))
            nc.sync.dma_start(out=w2_words[:, cols].bitcast(I32), in_=w2_word_rows[:, cols])

        load_x(0)
        nc.sync.dma_start(out=gain_row[0:1, :], in_=kva_norm_w.unsqueeze(0))
        for quadrant in range(4):
            nc.sync.dma_start(
                out=w1_planes[32 * quadrant : 32 * quadrant + 16, :].bitcast(I32),
                in_=w1_scale_rows[:, 4 * quadrant : 4 * quadrant + 4, :],
            )
        for g in range(0, X_PASSES, 2):
            nc.sync.dma_start(
                out=w1_words[:, g : g + 2, :].bitcast(I32),
                in_=w1_word_rows[g : g + 2, :, 0:LATENT].rearrange("g p w -> p g w"),
            )
        load_x(1)
        nc.sync.dma_start(
            out=w1_rope_words[:].bitcast(I32), in_=w1_word_rows[:, :, LATENT:].rearrange("g p w -> p g w")
        )
        load_x(2)
        for quadrant in range(4):
            nc.sync.dma_start(
                out=w2_planes[32 * quadrant : 32 * quadrant + 16, :].bitcast(I32),
                in_=w2_scale_rows[4 * quadrant : 4 * quadrant + 4, :].rearrange("r (j c) -> j r c", j=PLANES),
            )
        load_w2_words(0)
        load_w2_words(1)
        load_x(3)

        gain = keep.tile([P, PACK, P], F32)

        def spread_gain():
            gain_psum = wide_psum.tile([P, BANK], F32, tag="wide")
            nc.tensor.matmul(out=gain_psum[:], lhsT=ones[:], rhs=gain_row[:], start=True, stop=True)
            nc.vector.tensor_copy(out=gain[:], in_=gain_psum[:].rearrange("p (q t) -> p t q", t=PACK))

        def keep_clock(psum_tile, passes):
            for step in range(passes):
                nc.tensor.matmul(out=psum_tile[:], lhsT=idle[:, 0:P], rhs=idle[:], start=True, stop=True)

        def copy_out_of_psum(on_vector, out, in_):
            if on_vector:
                nc.vector.tensor_copy(out=out, in_=in_)
            else:
                nc.scalar.copy(out=out, in_=in_)

        def transpose_x(i, passes):
            pairs = x_sb[i][:].bitcast(F32)
            x_t = wide_psum.tile([P, len(passes), 2, P], F32, tag="wide")
            for index, g in enumerate(passes):
                for u in range(2):
                    nc.tensor.transpose(x_t[:, index, u, :], pairs[:, 256 * g + u : 256 * (g + 1) : 2], ident_f32[:])
            return x_t

        def group_x(i, passes, x_t, on_vector):
            copy_out_of_psum(
                on_vector,
                out=x_grouped[i][:, passes[0] : passes[-1] + 1, :, :].bitcast(F32),
                in_=x_t[:].rearrange("p g u k -> p g k u"),
            )

        def quantise_x(i, passes):
            cols = slice(P * passes[0], P * (passes[-1] + 1))
            nc.vector.quantize_mx(
                out=x_codes[i][:, cols].bitcast(FP8X4),
                scales=x_scales[i][:, cols],
                in_=x_grouped[i][:, passes[0] : passes[-1] + 1, :, :].rearrange("p g k t -> p (g k t)"),
            )

        def first_passes(i, acc, words, cols):
            for g in range(X_PASSES):
                tokens = slice(P * g, P * (g + 1))
                nc.tensor.matmul_mx(
                    out=acc[:],
                    lhsT=x_codes[i][:, tokens].bitcast(FP8X4),
                    lhsT_scale=x_scales[i][:, tokens],
                    rhs=words[:, g, :].bitcast(FP8X4),
                    rhs_scale=w1_planes[4 * g : P, cols],
                    start=(g == 0),
                    stop=(g == X_PASSES - 1),
                )

        def latent_matmul(i):
            latent = latent_psum.tile([P, LATENT], F32, tag="latent")
            first_passes(i, latent, w1_words, slice(0, LATENT))
            return latent

        def rope_matmul(i):
            raw_rope = narrow_psum.tile([P, ROPE], F32, tag="narrow")
            first_passes(i, raw_rope, w1_rope_words, slice(LATENT, A_COLS))
            return raw_rope

        def rotate_products(raw_rope):
            by_parity = raw_rope[:].rearrange("p (j e) -> p e j", e=2)
            from_even = work.tile([P, 2, HALF], F32)
            nc.vector.tensor_tensor(
                out=from_even[:], in0=by_parity[:, 0:1, :].to_broadcast([P, 2, HALF]), in1=table[:, 0:2, :], op=ALU.mult
            )
            from_odd = work.tile([P, 2, HALF], F32)
            nc.vector.tensor_tensor(
                out=from_odd[:], in0=by_parity[:, 1:2, :].to_broadcast([P, 2, HALF]), in1=table[:, 2:4, :], op=ALU.mult
            )
            return from_even, from_odd

        def rotate_sum(from_even, from_odd):
            rotated = work.tile([P, HALF, 2], F32)
            nc.vector.tensor_tensor(
                out=rotated[:],
                in0=from_even[:].rearrange("p e j -> p j e"),
                in1=from_odd[:].rearrange("p e j -> p j e"),
                op=ALU.add,
            )
            return rotated

        def repeat_rotated(i, rotated):
            for first_head in range(0, HEADS, HALF_HEADS):
                nc.gpsimd.tensor_scalar(
                    out=k_sb[i][:, first_head : first_head + HALF_HEADS, HEAD_DIM:],
                    in0=rotated[:].rearrange("p j e -> p (j e)").unsqueeze(1).to_broadcast([P, HALF_HEADS, ROPE]),
                    scalar1=1.0,
                    scalar2=0.0,
                    op0=ALU.mult,
                    op1=ALU.add,
                )

        def inverse_rms(latent):
            squares = work.tile([P, LATENT], BF16)
            sum_squares = work.tile([P, 1], F32)
            nc.scalar.activation(out=squares[:], in_=latent[:], func=ACT.Square, accum_out=sum_squares[:])
            inv_rms = work.tile([P, 1], F32)
            nc.scalar.activation(
                out=inv_rms[:], in_=sum_squares[:], func=ACT.Abs_reciprocal_sqrt, scale=1.0 / LATENT, bias=EPS
            )
            return inv_rms

        def scale_c(latent, inv_rms):
            c_sb = work.tile([P, PACK, P], BF16)
            nc.vector.scalar_tensor_tensor(
                out=c_sb[:],
                in0=latent[:].rearrange("p (q t) -> p t q", t=PACK),
                scalar=inv_rms[:],
                in1=gain[:],
                op0=ALU.mult,
                op1=ALU.mult,
            )
            return c_sb

        def transpose_c(c_sb):
            c_t = narrow_psum.tile([P, PACK, P], BF16, tag="narrow")
            for t in range(PACK):
                nc.tensor.transpose(c_t[:, t, :], c_sb[:, t, :], ident_bf16[:])
            return c_t

        def quantise_c(i, c_t):
            c_grouped = work.tile([P, P, PACK], BF16, align_bytes=64)
            nc.vector.tensor_copy(out=c_grouped[:], in_=c_t[:].rearrange("p t k -> p k t"))
            nc.vector.quantize_mx(
                out=c_codes[i][:].bitcast(FP8X4),
                scales=c_scales[i][:],
                in_=c_grouped[:].rearrange("p k t -> p (k t)"),
            )

        def second_matmul(i, first_bank, banks):
            for bank in range(first_bank, first_bank + banks):
                kv = wide_psum.tile([P, HEADS_PER_BANK, 2, HEAD_DIM], F32, tag="wide")
                plane = (BANK * bank) // PLANE_COLS
                plane_cols = slice((BANK * bank) % PLANE_COLS, (BANK * bank) % PLANE_COLS + BANK)
                nc.tensor.matmul_mx(
                    out=kv[:].rearrange("p h s d -> p (h s d)"),
                    lhsT=c_codes[i][:].bitcast(FP8X4),
                    lhsT_scale=c_scales[i][:],
                    rhs=w2_words[:, BANK * bank : BANK * (bank + 1)].bitcast(FP8X4),
                    rhs_scale=w2_planes[4 * plane : P, plane_cols],
                    start=True,
                    stop=True,
                )
                heads = slice(HEADS_PER_BANK * bank, HEADS_PER_BANK * (bank + 1))
                on_vector = bank in VECTOR_BANKS
                copy_out_of_psum(on_vector, out=k_sb[i][:, heads, 0:HEAD_DIM], in_=kv[:, :, 0, :])
                copy_out_of_psum(on_vector, out=v_sb[i][:, heads, :], in_=kv[:, :, 1, :])

        def store(i, first_head, heads_stored):
            stored = slice(first_head, first_head + heads_stored)
            nc.sync.dma_start(
                out=out_0[i, :, stored, :].rearrange("t h d -> t (h d)"),
                in_=k_sb[i][:, stored, :].rearrange("p h d -> p (h d)"),
            )
            nc.sync.dma_start(
                out=out_1[i, :, stored, :].rearrange("t h d -> t (h d)"),
                in_=v_sb[i][:, stored, :].rearrange("p h d -> p (h d)"),
            )

        clock_bank = latent_psum.tile([P, LATENT], F32, tag="latent")
        keep_clock(clock_bank, 6)
        for g in range(X_PASSES):
            group_x(0, [g], transpose_x(0, [g]), g % 2 == 0)
            quantise_x(0, [g])
            if g % 2 == 1:
                keep_clock(clock_bank, 1)
        finish_tables()
        spread_gain()
        latent = latent_matmul(0)
        clock_bank = wide_psum.tile([P, BANK], F32, tag="wide")
        keep_clock(clock_bank, 1)
        inv_rms = inverse_rms(latent)
        for passes in HALVES:
            group_x(1, passes, transpose_x(1, passes), False)
        raw_rope = rope_matmul(0)
        clock_bank = wide_psum.tile([P, BANK], F32, tag="wide")
        keep_clock(clock_bank, 2)
        c_sb = scale_c(latent, inv_rms)
        from_even, from_odd = rotate_products(raw_rope)

        for i in range(TILES):
            x_ts = []
            if i == 0:
                x_ts.append(transpose_x(2, HALVES[0]))
            c_t = transpose_c(c_sb)
            if i == 0:
                x_ts.append(transpose_x(2, HALVES[1]))
                for passes in HALVES:
                    quantise_x(1, passes)
            quantise_c(i, c_t)
            rotated = rotate_sum(from_even, from_odd)
            repeat_rotated(i, rotated)
            for passes, x_t in zip(HALVES, x_ts):
                group_x(2, passes, x_t, False)
            if i + 1 < TILES:
                latent = latent_matmul(i + 1)
            if i == 0:
                second_matmul(i, 0, 2)
                store(i, 0, 4)
                raw_rope = rope_matmul(1)
                inv_rms = inverse_rms(latent)
                second_matmul(i, 2, 2)
                store(i, 4, 4)
                from_even, from_odd = rotate_products(raw_rope)
            else:
                if i + 1 < TILES:
                    raw_rope = rope_matmul(i + 1)
                    inv_rms = inverse_rms(latent)
                    from_even, from_odd = rotate_products(raw_rope)
                second_matmul(i, 0, 4)
                if i < TILES_STORED_BY_HALVES:
                    store(i, 0, HALF_HEADS)
            if i + 1 < TILES:
                c_sb = scale_c(latent, inv_rms)
            if i == 0:
                for passes in HALVES:
                    quantise_x(2, passes)
            if i == 1:
                for passes in HALVES:
                    group_x(3, passes, transpose_x(3, passes), passes == HALVES[0])
                for passes in HALVES:
                    quantise_x(3, passes)
            second_matmul(i, 4, 4)
            if i < TILES_STORED_BY_HALVES:
                store(i, HALF_HEADS, HALF_HEADS)
            else:
                store(i, 0, HEADS)
